import numpy as np
import ml_dtypes


def mxq(x, axis, fmt="e4m3"):
    dtype, down = {"e4m3": (ml_dtypes.float8_e4m3fn, 7), "e5m2": (ml_dtypes.float8_e5m2, 14)}[fmt]
    v = np.moveaxis(np.asarray(x, np.float32).astype(ml_dtypes.bfloat16).astype(np.float64), axis, -1)
    blocks = v.reshape(v.shape[:-1] + (-1, 32))
    amax = np.abs(blocks).max(-1, keepdims=True)
    byte = np.maximum(np.where(amax > 0, np.frexp(amax)[1] - 1 + 127, 0) - down, 1)
    scale = np.exp2(byte - 127.0)
    codes = (blocks / scale).astype(np.float32).astype(dtype).astype(np.float64)
    return np.moveaxis((codes * scale).reshape(v.shape), -1, axis)


WIDE = False


def mx_kscale(k):
    if not WIDE:
        return np.ones(k)
    levels = np.array([10, -10, 5, -5, 0])
    a = np.random.permutation(np.resize(levels, k // 512 * 4)).reshape(k // 512, 4)
    idx = np.arange(k)
    return np.exp2(a[idx // 512, idx % 128 // 32])


BF16 = ml_dtypes.bfloat16


def bf(x):
    return np.asarray(x, np.float32).astype(BF16)


def f64(x):
    return np.asarray(x).astype(np.float64)


E2M1 = np.array([0.0, 0.5, 1.0, 1.5, 2.0, 3.0, 4.0, 6.0, -0.0, -0.5, -1.0, -1.5, -2.0, -3.0, -4.0, -6.0])


def pack_weight(w, fmt):
    k, n = w.shape
    w = f64(bf(w)).reshape(k // 32, 32, n)
    amax = np.abs(w).max(1)
    if fmt == "e4m3":
        byte = np.frexp(amax)[1] - 1 + 127 - 7
    else:
        mant, ex = np.frexp(amax / 6.0)
        byte = np.where(mant > 0.5, ex, ex - 1) + 127
    byte = np.clip(np.where(amax > 0, byte, 1), 1, 254)
    scaled = (w * np.exp2(127.0 - byte)[:, None, :]).reshape(k, n).astype(np.float32)
    by_word = np.ascontiguousarray(scaled.reshape(k // 512, 128, 4, n).transpose(0, 1, 3, 2))
    if fmt == "e4m3":
        words = by_word.astype(ml_dtypes.float8_e4m3fn).view(np.uint8)
    else:
        c = by_word.astype(ml_dtypes.float4_e2m1fn).view(np.uint8) & 0xF
        words = c[..., 0::2] | (c[..., 1::2] << 4)
    return np.ascontiguousarray(words), np.ascontiguousarray(byte.astype(np.uint8).reshape(k // 512, 16, n))


def unpack_weight(words, scales, fmt):
    g, p, n, _ = words.shape
    if fmt == "e4m3":
        vals = np.ascontiguousarray(words).view(ml_dtypes.float8_e4m3fn).astype(np.float64)
    else:
        nib = np.empty((g, p, n, 4), np.uint8)
        nib[..., 0::2] = words & 0xF
        nib[..., 1::2] = words >> 4
        vals = E2M1[nib]
    vals = vals * np.repeat(np.exp2(scales.astype(np.float64) - 127.0), 8, axis=1)[..., None]
    return vals.transpose(0, 1, 3, 2).reshape(g * 512, n)

def pack4(w):
    words, scales = pack_weight(w, "e2m1")
    return words.reshape(words.shape[0], 128, -1), scales


def unpack4(words, scales):
    return unpack_weight(words.reshape(words.shape[0], 128, -1, 2), scales, "e2m1")


B, DS, HH, WW, HID, HL, REP, GRP = 4, 64, 64, 64, 128, 1024, 8, 4
C = 2 * DS
CN = REP * C


def elu(v):
    return np.where(v > 0.0, v, np.exp(np.minimum(v, 0.0)) - 1.0)


def neighbor_sum(x):
    xp = np.pad(x, ((0, 0), (0, 0), (1, 1), (1, 1)))
    full = sum(xp[:, :, di:di + HH, dj:dj + WW] for di in range(3) for dj in range(3))
    return full - x


def to_rows(t):
    return t.transpose(0, 2, 3, 1).reshape(B * HH * WW, t.shape[1])


def to_maps(r):
    return r.reshape(B, HH, WW, r.shape[1]).transpose(0, 3, 1, 2)


def setup_inputs():
    sc = mx_kscale(CN)[::REP]
    x_cat = bf(np.random.standard_normal((B, C, HH, WW)) * 0.4 * sc[None, :, None, None])
    w1 = np.random.standard_normal((HID, CN)) / np.sqrt(CN) / np.repeat(sc, REP)[None, :]
    words, scales = pack4(np.ascontiguousarray(w1.T))
    return {"x_cat": x_cat, "w1_words": words, "w1_scales": scales}


def reference(x_cat, w1_words, w1_scales):
    nbr = neighbor_sum(f64(x_cat))
    xn = np.repeat(nbr, REP, axis=1)
    z = mxq(to_rows(xn), 1, "e4m3") @ unpack4(w1_words, w1_scales)
    return to_maps(elu(z))

@@ -1,0 +1,190 @@
+from contextlib import ExitStack
+
+import concourse.mybir as mybir
+
+FLOPS = 2 * 4 * 64 * 64 * 1024 * 128
+
+BF16 = mybir.dt.bfloat16
+F32 = mybir.dt.float32
+I32 = mybir.dt.int32
+U32 = mybir.dt.uint32
+U8 = mybir.dt.uint8
+FP8X4 = mybir.dt.float8_e4m3fn_x4
+FP4X4 = mybir.dt.float4_e2m1fn_x4
+ADD = mybir.AluOpType.add
+MAX = mybir.AluOpType.max
+SUBTRACT = mybir.AluOpType.subtract
+EXP = mybir.ActivationFunctionType.Exp
+RELU = mybir.ActivationFunctionType.Relu
+
+P = 128
+PACK = 4
+IMAGES = 4
+SIDE = 64
+PASSES = 2
+HALF_CHANNELS = 64
+HID = 128
+
+CHUNK_ROWS = 16
+CHUNK = CHUNK_ROWS * SIDE
+CHUNKS_PER_IMAGE = SIDE // CHUNK_ROWS
+N_CHUNKS = IMAGES * CHUNKS_PER_IMAGE
+BANK = 512
+BANKS_PER_CHUNK = CHUNK // BANK
+PITCH = SIDE + 1
+
+QUANTISE_LAG = 2
+FINISH_LAG = 3
+
+
+def tile_qca_operator_deep_pa_t_kernel(tc, x_cat, w1_words, w1_scales, out):
+    nc = tc.nc
+    with ExitStack() as stack:
+        keep = stack.enter_context(tc.tile_pool(name="keep", bufs=1))
+        sums = stack.enter_context(tc.tile_pool(name="sums", bufs=2))
+        nbrs = stack.enter_context(tc.tile_pool(name="nbrs", bufs=3))
+        quads = stack.enter_context(tc.tile_pool(name="quads", bufs=4))
+        moving = stack.enter_context(tc.tile_pool(name="moving", bufs=4))
+        packed = stack.enter_context(tc.tile_pool(name="packed", bufs=3))
+        tails = stack.enter_context(tc.tile_pool(name="tails", bufs=5))
+        results = stack.enter_context(tc.tile_pool(name="results", bufs=3))
+        psum = stack.enter_context(tc.psum_pool(name="psum", bufs=6))
+
+        x_pad = keep.tile([P, IMAGES, SIDE + 2, SIDE], BF16, name="x_pad")
+        nc.vector.memset(x_pad[:, :, 0 :: SIDE + 1, :], 0.0)
+        col_sum = keep.tile([P, CHUNK_ROWS * PITCH + 2], F32, name="col_sum")
+        nc.vector.memset(col_sum[:], 0.0)
+        w_planes = keep.tile([P, PASSES, HID], U8, name="w_planes", align_bytes=64)
+        nc.vector.memset(w_planes[:].rearrange("p g n -> p (g n)").bitcast(I32), 0)
+        w_codes = keep.tile([P, PASSES, 2 * HID], U8, name="w_codes", align_bytes=64)
+
+        def load_image(b):
+            for g in range(PASSES):
+                nc.sync.dma_start(
+                    out=x_pad[g::PASSES, b, 1 : SIDE + 1, :].rearrange("c i j -> c (i j)"),
+                    in_=x_cat[b, g * HALF_CHANNELS : (g + 1) * HALF_CHANNELS].rearrange("c i j -> c (i j)"),
+                )
+
+        load_image(0)
+        for g in range(PASSES):
+            nc.sync.dma_start(out=w_codes[:, g, :].bitcast(I32), in_=w1_words[g].bitcast(I32))
+            for quadrant in range(4):
+                nc.sync.dma_start(
+                    out=w_planes[32 * quadrant : 32 * quadrant + 4, g, :].bitcast(I32),
+                    in_=w1_scales[g, 4 * quadrant : 4 * quadrant + 4, :].bitcast(I32),
+                )
+        for b in range(1, IMAGES):
+            load_image(b)
+
+        pair = {}
+        side = {}
+        nbr = {}
+        xn = {}
+        acc = {}
+        neg = {}
+        res = {}
+
+        def rows_of(flat):
+            return flat.rearrange("p (i j) -> p i j", j=SIDE)
+
+        def shifted_sums(first):
+            return col_sum[:, first : first + CHUNK_ROWS * PITCH].rearrange("p (i j) -> p i j", j=PITCH)[:, :, 0:SIDE]
+
+        def image_rows(k, shift):
+            b, part = divmod(k, CHUNKS_PER_IMAGE)
+            first = part * CHUNK_ROWS + shift
+            return x_pad[:, b, first : first + CHUNK_ROWS, :]
+
+        def add_above_and_below(k):
+            pair[k] = sums.tile([P, CHUNK], F32, name="pair")
+            nc.vector.tensor_tensor(out=rows_of(pair[k][:]), in0=image_rows(k, 0), in1=image_rows(k, 2), op=ADD)
+
+        def add_centre(k):
+            nc.vector.tensor_tensor(out=shifted_sums(1), in0=rows_of(pair[k][:]), in1=image_rows(k, 1), op=ADD)
+
+        def add_left_and_right(k):
+            side[k] = sums.tile([P, CHUNK], F32, name="side")
+            nc.vector.tensor_tensor(out=rows_of(side[k][:]), in0=shifted_sums(0), in1=shifted_sums(2), op=ADD)
+
+        def round_neighbour_sum(k):
+            nbr[k] = nbrs.tile([P, CHUNK], BF16, name="nbr")
+            nc.vector.tensor_tensor(out=nbr[k][:], in0=side[k][:], in1=pair[k][:], op=ADD)
+
+        def repeat(k, h):
+            quad = quads.tile([P, BANK * PACK], BF16, name="quad")
+            nc.scalar.copy(
+                out=quad[:].rearrange("p (w t) -> p w t", t=PACK),
+                in_=nbr[k][:, h * BANK : (h + 1) * BANK].unsqueeze(2).to_broadcast([P, BANK, PACK]),
+            )
+            xn[k, h] = moving.tile([P, PASSES * BANK * PACK], BF16, name="xn", align_bytes=64)
+            for g in range(PASSES):
+                nc.sync.dma_start(
+                    out=xn[k, h][:, g * BANK * PACK : (g + 1) * BANK * PACK],
+                    in_=quad[g::PASSES, :].unsqueeze(1).to_broadcast([HALF_CHANNELS, 2, BANK * PACK]),
+                )
+
+        def quantise_and_multiply(k, h):
+            codes = packed.tile([P, PASSES * BANK], U32, name="codes", align_bytes=64)
+            planes = packed.tile([P, PASSES * BANK], U8, name="planes", align_bytes=64)
+            nc.vector.quantize_mx(out=codes[:].bitcast(FP8X4), scales=planes[:], in_=xn[k, h][:])
+            acc[k, h] = psum.tile([HID, BANK], F32, name="acc")
+            for g in range(PASSES):
+                nc.tensor.matmul_mx(
+                    out=acc[k, h][:],
+                    lhsT=w_codes[:, g, :].bitcast(FP4X4),
+                    lhsT_scale=w_planes[:, g, :],
+                    rhs=codes[:, g * BANK : (g + 1) * BANK].bitcast(FP8X4),
+                    rhs_scale=planes[:, g * BANK : (g + 1) * BANK],
+                    start=(g == 0),
+                    stop=(g == PASSES - 1),
+                )
+            neg[k, h] = tails.tile([HID, BANK], F32, name="neg")
+            nc.scalar.activation(out=neg[k, h][:], in_=acc[k, h][:], func=EXP)
+            nc.scalar.activation(out=neg[k, h][:], in_=neg[k, h][:], func=RELU, bias=1.0, scale=-1.0)
+
+        def finish(k, h):
+            if h == 0:
+                res[k] = results.tile([HID, CHUNK], F32, name="res")
+            nc.vector.scalar_tensor_tensor(
+                out=res[k][:, h * BANK : (h + 1) * BANK],
+                in0=acc[k, h][:],
+                scalar=0.0,
+                in1=neg[k, h][:],
+                op0=MAX,
+                op1=SUBTRACT,
+            )
+
+        def store(k):
+            b, part = divmod(k, CHUNKS_PER_IMAGE)
+            first = part * CHUNK_ROWS
+            nc.sync.dma_start(
+                out=out[b, :, first : first + CHUNK_ROWS, :].rearrange("o i j -> o (i j)"), in_=res[k][:]
+            )
+
+        with tc.manual_schedule():
+            for j in range(N_CHUNKS + FINISH_LAG):
+                summing = j < N_CHUNKS
+                q = j - QUANTISE_LAG
+                quantising = 0 <= q < N_CHUNKS
+                f = j - FINISH_LAG
+                finishing = 0 <= f
+                if summing:
+                    add_above_and_below(j)
+                if quantising:
+                    quantise_and_multiply(q, 0)
+                if summing:
+                    add_centre(j)
+                if quantising:
+                    quantise_and_multiply(q, 1)
+                if summing:
+                    add_left_and_right(j)
+                if finishing:
+                    finish(f, 0)
+                if summing:
+                    round_neighbour_sum(j)
+                if finishing:
+                    finish(f, 1)
+                    store(f)
+                if summing:
+                    for h in range(BANKS_PER_CHUNK):
+                        repeat(j, h)

@@ -1,6 +1,7 @@
 from contextlib import ExitStack
 
 import concourse.mybir as mybir
+from concourse.masks import make_identity
 
 FLOPS = 2 * 4 * 64 * 64 * 1024 * 128
 
@@ -33,8 +34,14 @@ BANK = 512
 BANKS_PER_CHUNK = CHUNK // BANK
 PITCH = SIDE + 1
 
-QUANTISE_LAG = 2
-FINISH_LAG = 3
+TENSOR_ROWS = 6
+ROW_PAIRS = TENSOR_ROWS // 2
+PAIR = 2 * SIDE
+VECTOR_ROWS = CHUNK_ROWS - TENSOR_ROWS
+VECTOR_PIXELS = VECTOR_ROWS * SIDE
+
+QUANTISE_LAG = 3
+FINISH_LAG = 5
 
 
 def tile_qca_operator_deep_pa_t_kernel(tc, x_cat, w1_words, w1_scales, out):
@@ -44,28 +51,32 @@ def tile_qca_operator_deep_pa_t_kernel(tc, x_cat, w1_words, w1_scales, out):
         sums = stack.enter_context(tc.tile_pool(name="sums", bufs=2))
         nbrs = stack.enter_context(tc.tile_pool(name="nbrs", bufs=3))
         quads = stack.enter_context(tc.tile_pool(name="quads", bufs=4))
-        moving = stack.enter_context(tc.tile_pool(name="moving", bufs=4))
+        moving = stack.enter_context(tc.tile_pool(name="moving", bufs=6))
         packed = stack.enter_context(tc.tile_pool(name="packed", bufs=3))
-        tails = stack.enter_context(tc.tile_pool(name="tails", bufs=5))
+        tails = stack.enter_context(tc.tile_pool(name="tails", bufs=7))
         results = stack.enter_context(tc.tile_pool(name="results", bufs=3))
-        psum = stack.enter_context(tc.psum_pool(name="psum", bufs=6))
+        psum_flip = stack.enter_context(tc.psum_pool(name="psum_flip", bufs=1))
+        psum_nbr = stack.enter_context(tc.psum_pool(name="psum_nbr", bufs=1))
+        psum_acc = stack.enter_context(tc.psum_pool(name="psum_acc", bufs=6))
 
         x_pad = keep.tile([P, IMAGES, SIDE + 2, SIDE], BF16, name="x_pad")
         nc.vector.memset(x_pad[:, :, 0 :: SIDE + 1, :], 0.0)
-        col_sum = keep.tile([P, CHUNK_ROWS * PITCH + 2], F32, name="col_sum")
+        col_sum = keep.tile([P, VECTOR_ROWS * PITCH + 2], F32, name="col_sum")
         nc.vector.memset(col_sum[:], 0.0)
         w_planes = keep.tile([P, PASSES, HID], U8, name="w_planes", align_bytes=64)
         nc.vector.memset(w_planes[:].rearrange("p g n -> p (g n)").bitcast(I32), 0)
         w_codes = keep.tile([P, PASSES, 2 * HID], U8, name="w_codes", align_bytes=64)
 
-        def load_image(b):
+        def load_rows(b, first, count):
             for g in range(PASSES):
                 nc.sync.dma_start(
-                    out=x_pad[g::PASSES, b, 1 : SIDE + 1, :].rearrange("c i j -> c (i j)"),
-                    in_=x_cat[b, g * HALF_CHANNELS : (g + 1) * HALF_CHANNELS].rearrange("c i j -> c (i j)"),
+                    out=x_pad[g::PASSES, b, 1 + first : 1 + first + count, :].rearrange("c i j -> c (i j)"),
+                    in_=x_cat[b, g * HALF_CHANNELS : (g + 1) * HALF_CHANNELS, first : first + count, :].rearrange(
+                        "c i j -> c (i j)"
+                    ),
                 )
 
-        load_image(0)
+        load_rows(0, 0, CHUNK_ROWS)
         for g in range(PASSES):
             nc.sync.dma_start(out=w_codes[:, g, :].bitcast(I32), in_=w1_words[g].bitcast(I32))
             for quadrant in range(4):
@@ -73,12 +84,37 @@ def tile_qca_operator_deep_pa_t_kernel(tc, x_cat, w1_words, w1_scales, out):
                     out=w_planes[32 * quadrant : 32 * quadrant + 4, g, :].bitcast(I32),
                     in_=w1_scales[g, 4 * quadrant : 4 * quadrant + 4, :].bitcast(I32),
                 )
+        for part in range(1, CHUNKS_PER_IMAGE):
+            load_rows(0, part * CHUNK_ROWS, CHUNK_ROWS)
         for b in range(1, IMAGES):
-            load_image(b)
+            load_rows(b, 0, SIDE)
+
+        ident = keep.tile([P, P], BF16, name="ident")
+        make_identity(nc, ident[:])
+        same_col = keep.tile([P, SIDE + 2], BF16, name="same_col")
+        nc.vector.memset(same_col[:], 0.0)
+        nc.vector.tensor_tensor(out=same_col[:, 1 : SIDE + 1], in0=ident[:, 0:SIDE], in1=ident[:, SIDE:P], op=ADD)
+        beside = keep.tile([P, SIDE], BF16, name="beside")
+        nc.vector.tensor_tensor(out=beside[:], in0=same_col[:, 0:SIDE], in1=same_col[:, 2 : SIDE + 2], op=ADD)
+        around = keep.tile([P, SIDE], BF16, name="around")
+        nc.vector.tensor_tensor(out=around[:], in0=beside[:], in1=same_col[:, 1 : SIDE + 1], op=ADD)
+        from_upper = keep.tile([P, 2, SIDE], BF16, name="from_upper")
+        from_lower = keep.tile([P, 2, SIDE], BF16, name="from_lower")
+        nc.vector.memset(from_upper[:], 0.0)
+        nc.vector.memset(from_lower[:], 0.0)
+        top, bottom = slice(0, SIDE), slice(SIDE, P)
+        nc.vector.tensor_copy(out=from_upper[top, 0, :], in_=around[top, :])
+        nc.vector.tensor_copy(out=from_upper[bottom, 0, :], in_=beside[bottom, :])
+        nc.vector.tensor_copy(out=from_upper[bottom, 1, :], in_=around[bottom, :])
+        nc.vector.tensor_copy(out=from_lower[top, 0, :], in_=around[top, :])
+        nc.vector.tensor_copy(out=from_lower[top, 1, :], in_=beside[top, :])
+        nc.vector.tensor_copy(out=from_lower[bottom, 1, :], in_=around[bottom, :])
 
         pair = {}
         side = {}
         nbr = {}
+        flipped = {}
+        nbr_acc = {}
         xn = {}
         acc = {}
         neg = {}
@@ -88,34 +124,68 @@ def tile_qca_operator_deep_pa_t_kernel(tc, x_cat, w1_words, w1_scales, out):
             return flat.rearrange("p (i j) -> p i j", j=SIDE)
 
         def shifted_sums(first):
-            return col_sum[:, first : first + CHUNK_ROWS * PITCH].rearrange("p (i j) -> p i j", j=PITCH)[:, :, 0:SIDE]
+            return col_sum[:, first : first + VECTOR_ROWS * PITCH].rearrange("p (i j) -> p i j", j=PITCH)[:, :, 0:SIDE]
 
-        def image_rows(k, shift):
+        def padded_rows(k, first, count):
             b, part = divmod(k, CHUNKS_PER_IMAGE)
-            first = part * CHUNK_ROWS + shift
-            return x_pad[:, b, first : first + CHUNK_ROWS, :]
+            return x_pad[:, b, part * CHUNK_ROWS + first : part * CHUNK_ROWS + first + count, :]
 
         def add_above_and_below(k):
-            pair[k] = sums.tile([P, CHUNK], F32, name="pair")
-            nc.vector.tensor_tensor(out=rows_of(pair[k][:]), in0=image_rows(k, 0), in1=image_rows(k, 2), op=ADD)
+            pair[k] = sums.tile([P, VECTOR_PIXELS], F32, name="pair")
+            nc.vector.tensor_tensor(
+                out=rows_of(pair[k][:]), in0=padded_rows(k, 0, VECTOR_ROWS), in1=padded_rows(k, 2, VECTOR_ROWS), op=ADD
+            )
 
         def add_centre(k):
-            nc.vector.tensor_tensor(out=shifted_sums(1), in0=rows_of(pair[k][:]), in1=image_rows(k, 1), op=ADD)
+            nc.vector.tensor_tensor(
+                out=shifted_sums(1), in0=rows_of(pair[k][:]), in1=padded_rows(k, 1, VECTOR_ROWS), op=ADD
+            )
 
         def add_left_and_right(k):
-            side[k] = sums.tile([P, CHUNK], F32, name="side")
+            side[k] = sums.tile([P, VECTOR_PIXELS], F32, name="side")
             nc.vector.tensor_tensor(out=rows_of(side[k][:]), in0=shifted_sums(0), in1=shifted_sums(2), op=ADD)
 
         def round_neighbour_sum(k):
-            nbr[k] = nbrs.tile([P, CHUNK], BF16, name="nbr")
+            nbr[k] = nbrs.tile([P, VECTOR_PIXELS], BF16, name="nbr")
             nc.vector.tensor_tensor(out=nbr[k][:], in0=side[k][:], in1=pair[k][:], op=ADD)
+
+        def transpose_rows(k):
+            flipped[k] = psum_flip.tile([P, ROW_PAIRS + 1, P], BF16, name="flipped")
+            for t in range(ROW_PAIRS + 1):
+                nc.tensor.transpose(
+                    flipped[k][:, t, :],
+                    padded_rows(k, VECTOR_ROWS + 2 * t, 2).rearrange("p i j -> p (i j)"),
+                    ident[:],
+                )
+
+        def sum_on_tensor_engine(k):
+            blocks = nbrs.tile([P, ROW_PAIRS + 1, P], BF16, name="blocks")
+            nc.vector.tensor_copy(out=blocks[:], in_=flipped[k][:])
+            nbr_acc[k] = psum_nbr.tile([P, ROW_PAIRS * PAIR], F32, name="nbr_acc")
+            for t in range(ROW_PAIRS):
+                pixels = nbr_acc[k][:, t * PAIR : (t + 1) * PAIR]
+                nc.tensor.matmul(
+                    out=pixels, lhsT=blocks[:, t, :], rhs=from_upper[:].rearrange("p i j -> p (i j)"), start=True, stop=False
+                )
+                nc.tensor.matmul(
+                    out=pixels, lhsT=blocks[:, t + 1, :], rhs=from_lower[:].rearrange("p i j -> p (i j)"), start=False, stop=True
+                )
+
+        def four_fold(quad, first, values, count):
+            nc.scalar.copy(
+                out=quad[:, first * PACK : (first + count) * PACK].rearrange("p (w t) -> p w t", t=PACK),
+                in_=values.unsqueeze(2).to_broadcast([P, count, PACK]),
+            )
 
         def repeat(k, h):
             quad = quads.tile([P, BANK * PACK], BF16, name="quad")
-            nc.scalar.copy(
-                out=quad[:].rearrange("p (w t) -> p w t", t=PACK),
-                in_=nbr[k][:, h * BANK : (h + 1) * BANK].unsqueeze(2).to_broadcast([P, BANK, PACK]),
-            )
+            first = h * BANK
+            by_vector = max(0, min(VECTOR_PIXELS - first, BANK))
+            if by_vector > 0:
+                four_fold(quad, 0, nbr[k][:, first : first + by_vector], by_vector)
+            if by_vector < BANK:
+                start = first + by_vector - VECTOR_PIXELS
+                four_fold(quad, by_vector, nbr_acc[k][:, start : start + BANK - by_vector], BANK - by_vector)
             xn[k, h] = moving.tile([P, PASSES * BANK * PACK], BF16, name="xn", align_bytes=64)
             for g in range(PASSES):
                 nc.sync.dma_start(
@@ -127,7 +197,7 @@ def tile_qca_operator_deep_pa_t_kernel(tc, x_cat, w1_words, w1_scales, out):
             codes = packed.tile([P, PASSES * BANK], U32, name="codes", align_bytes=64)
             planes = packed.tile([P, PASSES * BANK], U8, name="planes", align_bytes=64)
             nc.vector.quantize_mx(out=codes[:].bitcast(FP8X4), scales=planes[:], in_=xn[k, h][:])
-            acc[k, h] = psum.tile([HID, BANK], F32, name="acc")
+            acc[k, h] = psum_acc.tile([HID, BANK], F32, name="acc")
             for g in range(PASSES):
                 nc.tensor.matmul_mx(
                     out=acc[k, h][:],
@@ -138,6 +208,8 @@ def tile_qca_operator_deep_pa_t_kernel(tc, x_cat, w1_words, w1_scales, out):
                     start=(g == 0),
                     stop=(g == PASSES - 1),
                 )
+
+        def negative_part(k, h):
             neg[k, h] = tails.tile([HID, BANK], F32, name="neg")
             nc.scalar.activation(out=neg[k, h][:], in_=acc[k, h][:], func=EXP)
             nc.scalar.activation(out=neg[k, h][:], in_=neg[k, h][:], func=RELU, bias=1.0, scale=-1.0)
@@ -162,6 +234,7 @@ def tile_qca_operator_deep_pa_t_kernel(tc, x_cat, w1_words, w1_scales, out):
             )
 
         with tc.manual_schedule():
+            transpose_rows(0)
             for j in range(N_CHUNKS + FINISH_LAG):
                 summing = j < N_CHUNKS
                 q = j - QUANTISE_LAG
@@ -174,6 +247,7 @@ def tile_qca_operator_deep_pa_t_kernel(tc, x_cat, w1_words, w1_scales, out):
                     quantise_and_multiply(q, 0)
                 if summing:
                     add_centre(j)
+                    sum_on_tensor_engine(j)
                 if quantising:
                     quantise_and_multiply(q, 1)
                 if summing:
@@ -188,3 +262,8 @@ def tile_qca_operator_deep_pa_t_kernel(tc, x_cat, w1_words, w1_scales, out):
                 if summing:
                     for h in range(BANKS_PER_CHUNK):
                         repeat(j, h)
+                if quantising:
+                    for h in range(BANKS_PER_CHUNK):
+                        negative_part(q, h)
+                if j + 1 < N_CHUNKS:
+                    transpose_rows(j + 1)

@@ -23,7 +23,7 @@ PACK = 4
 IMAGES = 4
 SIDE = 64
 PASSES = 2
-HALF_CHANNELS = 64
+PASS_CHANNELS = 64
 HID = 128
 
 CHUNK_ROWS = 16
@@ -40,8 +40,8 @@ PAIR = 2 * SIDE
 VECTOR_ROWS = CHUNK_ROWS - TENSOR_ROWS
 VECTOR_PIXELS = VECTOR_ROWS * SIDE
 
-QUANTISE_LAG = 3
-FINISH_LAG = 5
+QUANTISE_LAG = 2
+FINISH_LAG = 4
 
 
 def tile_qca_operator_deep_pa_t_kernel(tc, x_cat, w1_words, w1_scales, out):
@@ -50,28 +50,28 @@ def tile_qca_operator_deep_pa_t_kernel(tc, x_cat, w1_words, w1_scales, out):
         keep = stack.enter_context(tc.tile_pool(name="keep", bufs=1))
         sums = stack.enter_context(tc.tile_pool(name="sums", bufs=2))
         nbrs = stack.enter_context(tc.tile_pool(name="nbrs", bufs=3))
-        quads = stack.enter_context(tc.tile_pool(name="quads", bufs=4))
-        moving = stack.enter_context(tc.tile_pool(name="moving", bufs=6))
+        quads = stack.enter_context(tc.tile_pool(name="quads", bufs=2 * BANKS_PER_CHUNK))
+        moving = stack.enter_context(tc.tile_pool(name="moving", bufs=(QUANTISE_LAG + 1) * BANKS_PER_CHUNK))
         packed = stack.enter_context(tc.tile_pool(name="packed", bufs=3))
-        tails = stack.enter_context(tc.tile_pool(name="tails", bufs=7))
+        tails = stack.enter_context(tc.tile_pool(name="tails", bufs=FINISH_LAG - QUANTISE_LAG + 1))
         results = stack.enter_context(tc.tile_pool(name="results", bufs=3))
         psum_flip = stack.enter_context(tc.psum_pool(name="psum_flip", bufs=1))
         psum_nbr = stack.enter_context(tc.psum_pool(name="psum_nbr", bufs=1))
-        psum_acc = stack.enter_context(tc.psum_pool(name="psum_acc", bufs=6))
+        psum_acc = stack.enter_context(tc.psum_pool(name="psum_acc", bufs=3 * BANKS_PER_CHUNK))
 
         x_pad = keep.tile([P, IMAGES, SIDE + 2, SIDE], BF16, name="x_pad")
         nc.vector.memset(x_pad[:, :, 0 :: SIDE + 1, :], 0.0)
         col_sum = keep.tile([P, VECTOR_ROWS * PITCH + 2], F32, name="col_sum")
         nc.vector.memset(col_sum[:], 0.0)
+        w_codes = keep.tile([P, PASSES, 2 * HID], U8, name="w_codes", align_bytes=64)
         w_planes = keep.tile([P, PASSES, HID], U8, name="w_planes", align_bytes=64)
         nc.vector.memset(w_planes[:].rearrange("p g n -> p (g n)").bitcast(I32), 0)
-        w_codes = keep.tile([P, PASSES, 2 * HID], U8, name="w_codes", align_bytes=64)
 
         def load_rows(b, first, count):
             for g in range(PASSES):
                 nc.sync.dma_start(
                     out=x_pad[g::PASSES, b, 1 + first : 1 + first + count, :].rearrange("c i j -> c (i j)"),
-                    in_=x_cat[b, g * HALF_CHANNELS : (g + 1) * HALF_CHANNELS, first : first + count, :].rearrange(
+                    in_=x_cat[b, g * PASS_CHANNELS : (g + 1) * PASS_CHANNELS, first : first + count, :].rearrange(
                         "c i j -> c (i j)"
                     ),
                 )
@@ -102,16 +102,16 @@ def tile_qca_operator_deep_pa_t_kernel(tc, x_cat, w1_words, w1_scales, out):
         from_lower = keep.tile([P, 2, SIDE], BF16, name="from_lower")
         nc.vector.memset(from_upper[:], 0.0)
         nc.vector.memset(from_lower[:], 0.0)
-        top, bottom = slice(0, SIDE), slice(SIDE, P)
-        nc.vector.tensor_copy(out=from_upper[top, 0, :], in_=around[top, :])
-        nc.vector.tensor_copy(out=from_upper[bottom, 0, :], in_=beside[bottom, :])
-        nc.vector.tensor_copy(out=from_upper[bottom, 1, :], in_=around[bottom, :])
-        nc.vector.tensor_copy(out=from_lower[top, 0, :], in_=around[top, :])
-        nc.vector.tensor_copy(out=from_lower[top, 1, :], in_=beside[top, :])
-        nc.vector.tensor_copy(out=from_lower[bottom, 1, :], in_=around[bottom, :])
+        upper_row, lower_row = slice(0, SIDE), slice(SIDE, P)
+        nc.vector.tensor_copy(out=from_upper[upper_row, 0, :], in_=around[upper_row, :])
+        nc.vector.tensor_copy(out=from_upper[lower_row, 0, :], in_=beside[lower_row, :])
+        nc.vector.tensor_copy(out=from_upper[lower_row, 1, :], in_=around[lower_row, :])
+        nc.vector.tensor_copy(out=from_lower[upper_row, 0, :], in_=around[upper_row, :])
+        nc.vector.tensor_copy(out=from_lower[upper_row, 1, :], in_=beside[upper_row, :])
+        nc.vector.tensor_copy(out=from_lower[lower_row, 1, :], in_=around[lower_row, :])
 
-        pair = {}
-        side = {}
+        above_below = {}
+        left_right = {}
         nbr = {}
         flipped = {}
         nbr_acc = {}
@@ -123,7 +123,7 @@ def tile_qca_operator_deep_pa_t_kernel(tc, x_cat, w1_words, w1_scales, out):
         def rows_of(flat):
             return flat.rearrange("p (i j) -> p i j", j=SIDE)
 
-        def shifted_sums(first):
+        def column_sums(first):
             return col_sum[:, first : first + VECTOR_ROWS * PITCH].rearrange("p (i j) -> p i j", j=PITCH)[:, :, 0:SIDE]
 
         def padded_rows(k, first, count):
@@ -131,23 +131,26 @@ def tile_qca_operator_deep_pa_t_kernel(tc, x_cat, w1_words, w1_scales, out):
             return x_pad[:, b, part * CHUNK_ROWS + first : part * CHUNK_ROWS + first + count, :]
 
         def add_above_and_below(k):
-            pair[k] = sums.tile([P, VECTOR_PIXELS], F32, name="pair")
+            above_below[k] = sums.tile([P, VECTOR_PIXELS], F32, name="above_below")
             nc.vector.tensor_tensor(
-                out=rows_of(pair[k][:]), in0=padded_rows(k, 0, VECTOR_ROWS), in1=padded_rows(k, 2, VECTOR_ROWS), op=ADD
+                out=rows_of(above_below[k][:]),
+                in0=padded_rows(k, 0, VECTOR_ROWS),
+                in1=padded_rows(k, 2, VECTOR_ROWS),
+                op=ADD,
             )
 
         def add_centre(k):
             nc.vector.tensor_tensor(
-                out=shifted_sums(1), in0=rows_of(pair[k][:]), in1=padded_rows(k, 1, VECTOR_ROWS), op=ADD
+                out=column_sums(1), in0=rows_of(above_below[k][:]), in1=padded_rows(k, 1, VECTOR_ROWS), op=ADD
             )
 
         def add_left_and_right(k):
-            side[k] = sums.tile([P, VECTOR_PIXELS], F32, name="side")
-            nc.vector.tensor_tensor(out=rows_of(side[k][:]), in0=shifted_sums(0), in1=shifted_sums(2), op=ADD)
+            left_right[k] = sums.tile([P, VECTOR_PIXELS], F32, name="left_right")
+            nc.vector.tensor_tensor(out=rows_of(left_right[k][:]), in0=column_sums(0), in1=column_sums(2), op=ADD)
 
-        def round_neighbour_sum(k):
+        def add_up_and_round(k):
             nbr[k] = nbrs.tile([P, VECTOR_PIXELS], BF16, name="nbr")
-            nc.vector.tensor_tensor(out=nbr[k][:], in0=side[k][:], in1=pair[k][:], op=ADD)
+            nc.vector.tensor_tensor(out=nbr[k][:], in0=left_right[k][:], in1=above_below[k][:], op=ADD)
 
         def transpose_rows(k):
             flipped[k] = psum_flip.tile([P, ROW_PAIRS + 1, P], BF16, name="flipped")
@@ -165,10 +168,18 @@ def tile_qca_operator_deep_pa_t_kernel(tc, x_cat, w1_words, w1_scales, out):
             for t in range(ROW_PAIRS):
                 pixels = nbr_acc[k][:, t * PAIR : (t + 1) * PAIR]
                 nc.tensor.matmul(
-                    out=pixels, lhsT=blocks[:, t, :], rhs=from_upper[:].rearrange("p i j -> p (i j)"), start=True, stop=False
+                    out=pixels,
+                    lhsT=blocks[:, t, :],
+                    rhs=from_upper[:].rearrange("p i j -> p (i j)"),
+                    start=True,
+                    stop=False,
                 )
                 nc.tensor.matmul(
-                    out=pixels, lhsT=blocks[:, t + 1, :], rhs=from_lower[:].rearrange("p i j -> p (i j)"), start=False, stop=True
+                    out=pixels,
+                    lhsT=blocks[:, t + 1, :],
+                    rhs=from_lower[:].rearrange("p i j -> p (i j)"),
+                    start=False,
+                    stop=True,
                 )
 
         def four_fold(quad, first, values, count):
@@ -184,13 +195,13 @@ def tile_qca_operator_deep_pa_t_kernel(tc, x_cat, w1_words, w1_scales, out):
             if by_vector > 0:
                 four_fold(quad, 0, nbr[k][:, first : first + by_vector], by_vector)
             if by_vector < BANK:
-                start = first + by_vector - VECTOR_PIXELS
-                four_fold(quad, by_vector, nbr_acc[k][:, start : start + BANK - by_vector], BANK - by_vector)
+                skipped = first + by_vector - VECTOR_PIXELS
+                four_fold(quad, by_vector, nbr_acc[k][:, skipped : skipped + BANK - by_vector], BANK - by_vector)
             xn[k, h] = moving.tile([P, PASSES * BANK * PACK], BF16, name="xn", align_bytes=64)
             for g in range(PASSES):
                 nc.sync.dma_start(
                     out=xn[k, h][:, g * BANK * PACK : (g + 1) * BANK * PACK],
-                    in_=quad[g::PASSES, :].unsqueeze(1).to_broadcast([HALF_CHANNELS, 2, BANK * PACK]),
+                    in_=quad[g::PASSES, :].unsqueeze(1).to_broadcast([PASS_CHANNELS, 2, BANK * PACK]),
                 )
 
         def quantise_and_multiply(k, h):
@@ -209,21 +220,18 @@ def tile_qca_operator_deep_pa_t_kernel(tc, x_cat, w1_words, w1_scales, out):
                     stop=(g == PASSES - 1),
                 )
 
-        def negative_part(k, h):
-            neg[k, h] = tails.tile([HID, BANK], F32, name="neg")
-            nc.scalar.activation(out=neg[k, h][:], in_=acc[k, h][:], func=EXP)
-            nc.scalar.activation(out=neg[k, h][:], in_=neg[k, h][:], func=RELU, bias=1.0, scale=-1.0)
+        def negative_part(k):
+            neg[k] = tails.tile([HID, CHUNK], F32, name="neg")
+            for h in range(BANKS_PER_CHUNK):
+                nc.scalar.activation(out=neg[k][:, h * BANK : (h + 1) * BANK], in_=acc[k, h][:], func=EXP)
+            nc.scalar.activation(out=neg[k][:], in_=neg[k][:], func=RELU, bias=1.0, scale=-1.0)
 
         def finish(k, h):
             if h == 0:
                 res[k] = results.tile([HID, CHUNK], F32, name="res")
+            bank = slice(h * BANK, (h + 1) * BANK)
             nc.vector.scalar_tensor_tensor(
-                out=res[k][:, h * BANK : (h + 1) * BANK],
-                in0=acc[k, h][:],
-                scalar=0.0,
-                in1=neg[k, h][:],
-                op0=MAX,
-                op1=SUBTRACT,
+                out=res[k][:, bank], in0=acc[k, h][:], scalar=0.0, in1=neg[k][:, bank], op0=MAX, op1=SUBTRACT
             )
 
         def store(k):
@@ -243,27 +251,22 @@ def tile_qca_operator_deep_pa_t_kernel(tc, x_cat, w1_words, w1_scales, out):
                 finishing = 0 <= f
                 if summing:
                     add_above_and_below(j)
-                if quantising:
-                    quantise_and_multiply(q, 0)
-                if summing:
-                    add_centre(j)
-                    sum_on_tensor_engine(j)
-                if quantising:
-                    quantise_and_multiply(q, 1)
-                if summing:
-                    add_left_and_right(j)
                 if finishing:
                     finish(f, 0)
                 if summing:
-                    round_neighbour_sum(j)
+                    add_centre(j)
+                    sum_on_tensor_engine(j)
+                    add_left_and_right(j)
                 if finishing:
                     finish(f, 1)
                     store(f)
                 if summing:
+                    add_up_and_round(j)
                     for h in range(BANKS_PER_CHUNK):
                         repeat(j, h)
                 if quantising:
                     for h in range(BANKS_PER_CHUNK):
-                        negative_part(q, h)
+                        quantise_and_multiply(q, h)
+                    negative_part(q)
                 if j + 1 < N_CHUNKS:
                     transpose_rows(j + 1)

@@ -39,9 +39,10 @@ ROW_PAIRS = TENSOR_ROWS // 2
 PAIR = 2 * SIDE
 VECTOR_ROWS = CHUNK_ROWS - TENSOR_ROWS
 VECTOR_PIXELS = VECTOR_ROWS * SIDE
+TENSOR_PIXELS = TENSOR_ROWS * SIDE
 
-QUANTISE_LAG = 2
-FINISH_LAG = 4
+QUANTISE_LAG = 3
+FINISH_LAG = 5
 
 
 def tile_qca_operator_deep_pa_t_kernel(tc, x_cat, w1_words, w1_scales, out):
@@ -54,7 +55,7 @@ def tile_qca_operator_deep_pa_t_kernel(tc, x_cat, w1_words, w1_scales, out):
         moving = stack.enter_context(tc.tile_pool(name="moving", bufs=(QUANTISE_LAG + 1) * BANKS_PER_CHUNK))
         packed = stack.enter_context(tc.tile_pool(name="packed", bufs=3))
         tails = stack.enter_context(tc.tile_pool(name="tails", bufs=FINISH_LAG - QUANTISE_LAG + 1))
-        results = stack.enter_context(tc.tile_pool(name="results", bufs=3))
+        results = stack.enter_context(tc.tile_pool(name="results", bufs=4))
         psum_flip = stack.enter_context(tc.psum_pool(name="psum_flip", bufs=1))
         psum_nbr = stack.enter_context(tc.psum_pool(name="psum_nbr", bufs=1))
         psum_acc = stack.enter_context(tc.psum_pool(name="psum_acc", bufs=3 * BANKS_PER_CHUNK))
@@ -115,10 +116,10 @@ def tile_qca_operator_deep_pa_t_kernel(tc, x_cat, w1_words, w1_scales, out):
         nbr = {}
         flipped = {}
         nbr_acc = {}
+        quad = {}
         xn = {}
         acc = {}
         neg = {}
-        res = {}
 
         def rows_of(flat):
             return flat.rearrange("p (i j) -> p i j", j=SIDE)
@@ -134,14 +135,17 @@ def tile_qca_operator_deep_pa_t_kernel(tc, x_cat, w1_words, w1_scales, out):
             above_below[k] = sums.tile([P, VECTOR_PIXELS], F32, name="above_below")
             nc.vector.tensor_tensor(
                 out=rows_of(above_below[k][:]),
-                in0=padded_rows(k, 0, VECTOR_ROWS),
-                in1=padded_rows(k, 2, VECTOR_ROWS),
+                in0=padded_rows(k, TENSOR_ROWS, VECTOR_ROWS),
+                in1=padded_rows(k, TENSOR_ROWS + 2, VECTOR_ROWS),
                 op=ADD,
             )
 
         def add_centre(k):
             nc.vector.tensor_tensor(
-                out=column_sums(1), in0=rows_of(above_below[k][:]), in1=padded_rows(k, 1, VECTOR_ROWS), op=ADD
+                out=column_sums(1),
+                in0=rows_of(above_below[k][:]),
+                in1=padded_rows(k, TENSOR_ROWS + 1, VECTOR_ROWS),
+                op=ADD,
             )
 
         def add_left_and_right(k):
@@ -157,7 +161,7 @@ def tile_qca_operator_deep_pa_t_kernel(tc, x_cat, w1_words, w1_scales, out):
             for t in range(ROW_PAIRS + 1):
                 nc.tensor.transpose(
                     flipped[k][:, t, :],
-                    padded_rows(k, VECTOR_ROWS + 2 * t, 2).rearrange("p i j -> p (i j)"),
+                    padded_rows(k, 2 * t, 2).rearrange("p i j -> p (i j)"),
                     ident[:],
                 )
 
@@ -182,27 +186,32 @@ def tile_qca_operator_deep_pa_t_kernel(tc, x_cat, w1_words, w1_scales, out):
                     stop=True,
                 )
 
-        def four_fold(quad, first, values, count):
+        def four_fold(k, first, values, count):
+            h, start = divmod(first, BANK)
+            if start == 0:
+                quad[k, h] = quads.tile([P, BANK * PACK], BF16, name="quad")
             nc.scalar.copy(
-                out=quad[:, first * PACK : (first + count) * PACK].rearrange("p (w t) -> p w t", t=PACK),
+                out=quad[k, h][:, start * PACK : (start + count) * PACK].rearrange("p (w t) -> p w t", t=PACK),
                 in_=values.unsqueeze(2).to_broadcast([P, count, PACK]),
             )
 
-        def repeat(k, h):
-            quad = quads.tile([P, BANK * PACK], BF16, name="quad")
-            first = h * BANK
-            by_vector = max(0, min(VECTOR_PIXELS - first, BANK))
-            if by_vector > 0:
-                four_fold(quad, 0, nbr[k][:, first : first + by_vector], by_vector)
-            if by_vector < BANK:
-                skipped = first + by_vector - VECTOR_PIXELS
-                four_fold(quad, by_vector, nbr_acc[k][:, skipped : skipped + BANK - by_vector], BANK - by_vector)
+        def spread(k, h):
             xn[k, h] = moving.tile([P, PASSES * BANK * PACK], BF16, name="xn", align_bytes=64)
             for g in range(PASSES):
                 nc.sync.dma_start(
                     out=xn[k, h][:, g * BANK * PACK : (g + 1) * BANK * PACK],
-                    in_=quad[g::PASSES, :].unsqueeze(1).to_broadcast([PASS_CHANNELS, 2, BANK * PACK]),
+                    in_=quad[k, h][g::PASSES, :].unsqueeze(1).to_broadcast([PASS_CHANNELS, 2, BANK * PACK]),
                 )
+
+        def repeat_tensor_rows(k):
+            four_fold(k, 0, nbr_acc[k][:], TENSOR_PIXELS)
+
+        def repeat_vector_rows(k):
+            rest = BANK - TENSOR_PIXELS
+            four_fold(k, TENSOR_PIXELS, nbr[k][:, 0:rest], rest)
+            spread(k, 0)
+            four_fold(k, BANK, nbr[k][:, rest:VECTOR_PIXELS], BANK)
+            spread(k, 1)
 
         def quantise_and_multiply(k, h):
             codes = packed.tile([P, PASSES * BANK], U32, name="codes", align_bytes=64)
@@ -220,26 +229,23 @@ def tile_qca_operator_deep_pa_t_kernel(tc, x_cat, w1_words, w1_scales, out):
                     stop=(g == PASSES - 1),
                 )
 
-        def negative_part(k):
+        def exponentials(k):
             neg[k] = tails.tile([HID, CHUNK], F32, name="neg")
             for h in range(BANKS_PER_CHUNK):
                 nc.scalar.activation(out=neg[k][:, h * BANK : (h + 1) * BANK], in_=acc[k, h][:], func=EXP)
+
+        def negative_part(k):
             nc.scalar.activation(out=neg[k][:], in_=neg[k][:], func=RELU, bias=1.0, scale=-1.0)
 
         def finish(k, h):
-            if h == 0:
-                res[k] = results.tile([HID, CHUNK], F32, name="res")
-            bank = slice(h * BANK, (h + 1) * BANK)
+            res = results.tile([HID, BANK], F32, name="res")
             nc.vector.scalar_tensor_tensor(
-                out=res[k][:, bank], in0=acc[k, h][:], scalar=0.0, in1=neg[k][:, bank], op0=MAX, op1=SUBTRACT
+                out=res[:], in0=acc[k, h][:], scalar=0.0, in1=neg[k][:, h * BANK : (h + 1) * BANK], op0=MAX, op1=SUBTRACT
             )
-
-        def store(k):
             b, part = divmod(k, CHUNKS_PER_IMAGE)
-            first = part * CHUNK_ROWS
-            nc.sync.dma_start(
-                out=out[b, :, first : first + CHUNK_ROWS, :].rearrange("o i j -> o (i j)"), in_=res[k][:]
-            )
+            bank_rows = BANK // SIDE
+            first = part * CHUNK_ROWS + h * bank_rows
+            nc.sync.dma_start(out=out[b, :, first : first + bank_rows, :].rearrange("o i j -> o (i j)"), in_=res[:])
 
         with tc.manual_schedule():
             transpose_rows(0)
@@ -251,22 +257,24 @@ def tile_qca_operator_deep_pa_t_kernel(tc, x_cat, w1_words, w1_scales, out):
                 finishing = 0 <= f
                 if summing:
                     add_above_and_below(j)
-                if finishing:
-                    finish(f, 0)
+                if quantising:
+                    quantise_and_multiply(q, 0)
                 if summing:
                     add_centre(j)
-                    sum_on_tensor_engine(j)
+                if quantising:
+                    quantise_and_multiply(q, 1)
+                    exponentials(q)
+                if summing:
                     add_left_and_right(j)
+                    sum_on_tensor_engine(j)
+                    repeat_tensor_rows(j)
+                if quantising:
+                    negative_part(q)
                 if finishing:
+                    finish(f, 0)
                     finish(f, 1)
-                    store(f)
                 if summing:
                     add_up_and_round(j)
-                    for h in range(BANKS_PER_CHUNK):
-                        repeat(j, h)
-                if quantising:
-                    for h in range(BANKS_PER_CHUNK):
-                        quantise_and_multiply(q, h)
-                    negative_part(q)
+                    repeat_vector_rows(j)
                 if j + 1 < N_CHUNKS:
                     transpose_rows(j + 1)

@@ -33,16 +33,21 @@ N_CHUNKS = IMAGES * CHUNKS_PER_IMAGE
 BANK = 512
 BANKS_PER_CHUNK = CHUNK // BANK
 PITCH = SIDE + 1
+BANK_ROWS = BANK // SIDE
 
-TENSOR_ROWS = 6
-ROW_PAIRS = TENSOR_ROWS // 2
-PAIR = 2 * SIDE
-VECTOR_ROWS = CHUNK_ROWS - TENSOR_ROWS
+PATCH_ROWS = 8
+PATCH_COLS = 16
+TENSOR_ROWS = PATCH_ROWS - 2
+STRIPS = 5
+STRIP_STEP = 12
+VECTOR_ROWS = BANK_ROWS - TENSOR_ROWS
+CHUNK_VECTOR_ROWS = VECTOR_ROWS * BANKS_PER_CHUNK
 VECTOR_PIXELS = VECTOR_ROWS * SIDE
 TENSOR_PIXELS = TENSOR_ROWS * SIDE
+PAD_ROWS = SIDE + BANK_ROWS
 
 QUANTISE_LAG = 3
-FINISH_LAG = 5
+FINISH_LAG = 4
 
 
 def tile_qca_operator_deep_pa_t_kernel(tc, x_cat, w1_words, w1_scales, out):
@@ -51,18 +56,20 @@ def tile_qca_operator_deep_pa_t_kernel(tc, x_cat, w1_words, w1_scales, out):
         keep = stack.enter_context(tc.tile_pool(name="keep", bufs=1))
         sums = stack.enter_context(tc.tile_pool(name="sums", bufs=2))
         nbrs = stack.enter_context(tc.tile_pool(name="nbrs", bufs=3))
+        strip_pool = stack.enter_context(tc.tile_pool(name="strip_pool", bufs=2))
+        patches = stack.enter_context(tc.tile_pool(name="patches", bufs=2 * BANKS_PER_CHUNK))
         quads = stack.enter_context(tc.tile_pool(name="quads", bufs=2 * BANKS_PER_CHUNK))
         moving = stack.enter_context(tc.tile_pool(name="moving", bufs=(QUANTISE_LAG + 1) * BANKS_PER_CHUNK))
         packed = stack.enter_context(tc.tile_pool(name="packed", bufs=3))
         tails = stack.enter_context(tc.tile_pool(name="tails", bufs=FINISH_LAG - QUANTISE_LAG + 1))
         results = stack.enter_context(tc.tile_pool(name="results", bufs=4))
-        psum_flip = stack.enter_context(tc.psum_pool(name="psum_flip", bufs=1))
-        psum_nbr = stack.enter_context(tc.psum_pool(name="psum_nbr", bufs=1))
-        psum_acc = stack.enter_context(tc.psum_pool(name="psum_acc", bufs=3 * BANKS_PER_CHUNK))
+        psum_flip = stack.enter_context(tc.psum_pool(name="psum_flip", bufs=BANKS_PER_CHUNK))
+        psum_nbr = stack.enter_context(tc.psum_pool(name="psum_nbr", bufs=BANKS_PER_CHUNK))
+        psum_acc = stack.enter_context(tc.psum_pool(name="psum_acc", bufs=2 * BANKS_PER_CHUNK))
 
-        x_pad = keep.tile([P, IMAGES, SIDE + 2, SIDE], BF16, name="x_pad")
-        nc.vector.memset(x_pad[:, :, 0 :: SIDE + 1, :], 0.0)
-        col_sum = keep.tile([P, VECTOR_ROWS * PITCH + 2], F32, name="col_sum")
+        x_pad = keep.tile([P, IMAGES, PAD_ROWS, SIDE], BF16, name="x_pad")
+        nc.vector.memset(x_pad[:, :, 0 : SIDE + 2 : SIDE + 1, :], 0.0)
+        col_sum = keep.tile([P, CHUNK_VECTOR_ROWS * PITCH + 2], F32, name="col_sum")
         nc.vector.memset(col_sum[:], 0.0)
         w_codes = keep.tile([P, PASSES, 2 * HID], U8, name="w_codes", align_bytes=64)
         w_planes = keep.tile([P, PASSES, HID], U8, name="w_planes", align_bytes=64)
@@ -92,28 +99,30 @@ def tile_qca_operator_deep_pa_t_kernel(tc, x_cat, w1_words, w1_scales, out):
 
         ident = keep.tile([P, P], BF16, name="ident")
         make_identity(nc, ident[:])
-        same_col = keep.tile([P, SIDE + 2], BF16, name="same_col")
-        nc.vector.memset(same_col[:], 0.0)
-        nc.vector.tensor_tensor(out=same_col[:, 1 : SIDE + 1], in0=ident[:, 0:SIDE], in1=ident[:, SIDE:P], op=ADD)
-        beside = keep.tile([P, SIDE], BF16, name="beside")
-        nc.vector.tensor_tensor(out=beside[:], in0=same_col[:, 0:SIDE], in1=same_col[:, 2 : SIDE + 2], op=ADD)
-        around = keep.tile([P, SIDE], BF16, name="around")
-        nc.vector.tensor_tensor(out=around[:], in0=beside[:], in1=same_col[:, 1 : SIDE + 1], op=ADD)
-        from_upper = keep.tile([P, 2, SIDE], BF16, name="from_upper")
-        from_lower = keep.tile([P, 2, SIDE], BF16, name="from_lower")
-        nc.vector.memset(from_upper[:], 0.0)
-        nc.vector.memset(from_lower[:], 0.0)
-        upper_row, lower_row = slice(0, SIDE), slice(SIDE, P)
-        nc.vector.tensor_copy(out=from_upper[upper_row, 0, :], in_=around[upper_row, :])
-        nc.vector.tensor_copy(out=from_upper[lower_row, 0, :], in_=beside[lower_row, :])
-        nc.vector.tensor_copy(out=from_upper[lower_row, 1, :], in_=around[lower_row, :])
-        nc.vector.tensor_copy(out=from_lower[upper_row, 0, :], in_=around[upper_row, :])
-        nc.vector.tensor_copy(out=from_lower[upper_row, 1, :], in_=beside[upper_row, :])
-        nc.vector.tensor_copy(out=from_lower[lower_row, 1, :], in_=around[lower_row, :])
+        ident_pad = keep.tile([P, PATCH_ROWS, PATCH_COLS + 2], BF16, name="ident_pad")
+        nc.vector.memset(ident_pad[:], 0.0)
+        nc.vector.tensor_copy(
+            out=ident_pad[:, :, 1 : PATCH_COLS + 1], in_=ident[:].rearrange("p (i j) -> p i j", j=PATCH_COLS)
+        )
+        beside = keep.tile([P, PATCH_ROWS, PATCH_COLS], BF16, name="beside")
+        nc.vector.tensor_tensor(
+            out=beside[:], in0=ident_pad[:, :, 0:PATCH_COLS], in1=ident_pad[:, :, 2 : PATCH_COLS + 2], op=ADD
+        )
+        around = keep.tile([P, PATCH_ROWS, PATCH_COLS], BF16, name="around")
+        nc.vector.tensor_tensor(out=around[:], in0=beside[:], in1=ident_pad[:, :, 1 : PATCH_COLS + 1], op=ADD)
+        outer = keep.tile([P, TENSOR_ROWS, PATCH_COLS], BF16, name="outer")
+        nc.vector.tensor_tensor(
+            out=outer[:], in0=around[:, 0:TENSOR_ROWS, :], in1=around[:, 2 : TENSOR_ROWS + 2, :], op=ADD
+        )
+        window = keep.tile([P, PATCH_COLS, TENSOR_ROWS], BF16, name="window")
+        nc.vector.tensor_tensor(
+            out=window[:].rearrange("p j o -> p o j"), in0=outer[:], in1=beside[:, 1 : TENSOR_ROWS + 1, :], op=ADD
+        )
 
         above_below = {}
         left_right = {}
         nbr = {}
+        strips = {}
         flipped = {}
         nbr_acc = {}
         quad = {}
@@ -122,78 +131,71 @@ def tile_qca_operator_deep_pa_t_kernel(tc, x_cat, w1_words, w1_scales, out):
         neg = {}
 
         def rows_of(flat):
-            return flat.rearrange("p (i j) -> p i j", j=SIDE)
+            return flat.rearrange("p (h r j) -> p h r j", h=BANKS_PER_CHUNK, j=SIDE)
 
         def column_sums(first):
-            return col_sum[:, first : first + VECTOR_ROWS * PITCH].rearrange("p (i j) -> p i j", j=PITCH)[:, :, 0:SIDE]
+            return col_sum[:, first : first + CHUNK_VECTOR_ROWS * PITCH].rearrange(
+                "p (h r j) -> p h r j", h=BANKS_PER_CHUNK, j=PITCH
+            )[:, :, :, 0:SIDE]
 
-        def padded_rows(k, first, count):
+        def padded_rows(k, offset):
             b, part = divmod(k, CHUNKS_PER_IMAGE)
-            return x_pad[:, b, part * CHUNK_ROWS + first : part * CHUNK_ROWS + first + count, :]
+            first = part * CHUNK_ROWS + TENSOR_ROWS + offset
+            return x_pad[:, b, first : first + CHUNK_ROWS, :].rearrange("p (h r) j -> p h r j", r=BANK_ROWS)[
+                :, :, 0:VECTOR_ROWS, :
+            ]
 
         def add_above_and_below(k):
-            above_below[k] = sums.tile([P, VECTOR_PIXELS], F32, name="above_below")
+            above_below[k] = sums.tile([P, CHUNK_VECTOR_ROWS * SIDE], F32, name="above_below")
             nc.vector.tensor_tensor(
-                out=rows_of(above_below[k][:]),
-                in0=padded_rows(k, TENSOR_ROWS, VECTOR_ROWS),
-                in1=padded_rows(k, TENSOR_ROWS + 2, VECTOR_ROWS),
-                op=ADD,
+                out=rows_of(above_below[k][:]), in0=padded_rows(k, 0), in1=padded_rows(k, 2), op=ADD
             )
 
         def add_centre(k):
-            nc.vector.tensor_tensor(
-                out=column_sums(1),
-                in0=rows_of(above_below[k][:]),
-                in1=padded_rows(k, TENSOR_ROWS + 1, VECTOR_ROWS),
-                op=ADD,
-            )
+            nc.vector.tensor_tensor(out=column_sums(1), in0=rows_of(above_below[k][:]), in1=padded_rows(k, 1), op=ADD)
 
         def add_left_and_right(k):
-            left_right[k] = sums.tile([P, VECTOR_PIXELS], F32, name="left_right")
+            left_right[k] = sums.tile([P, CHUNK_VECTOR_ROWS * SIDE], F32, name="left_right")
             nc.vector.tensor_tensor(out=rows_of(left_right[k][:]), in0=column_sums(0), in1=column_sums(2), op=ADD)
 
         def add_up_and_round(k):
-            nbr[k] = nbrs.tile([P, VECTOR_PIXELS], BF16, name="nbr")
+            nbr[k] = nbrs.tile([P, CHUNK_VECTOR_ROWS * SIDE], BF16, name="nbr")
             nc.vector.tensor_tensor(out=nbr[k][:], in0=left_right[k][:], in1=above_below[k][:], op=ADD)
 
-        def transpose_rows(k):
-            flipped[k] = psum_flip.tile([P, ROW_PAIRS + 1, P], BF16, name="flipped")
-            for t in range(ROW_PAIRS + 1):
-                nc.tensor.transpose(
-                    flipped[k][:, t, :],
-                    padded_rows(k, 2 * t, 2).rearrange("p i j -> p (i j)"),
-                    ident[:],
-                )
+        def copy_strip(b, s, first, count):
+            if b not in strips:
+                strips[b] = strip_pool.tile([P, STRIPS, SIDE, PATCH_COLS], BF16, name="strips")
+            nc.vector.tensor_copy(
+                out=strips[b][:, s, first : first + count, :],
+                in_=x_pad[:, b, first : first + count, s * STRIP_STEP : s * STRIP_STEP + PATCH_COLS],
+            )
 
-        def sum_on_tensor_engine(k):
-            blocks = nbrs.tile([P, ROW_PAIRS + 1, P], BF16, name="blocks")
-            nc.vector.tensor_copy(out=blocks[:], in_=flipped[k][:])
-            nbr_acc[k] = psum_nbr.tile([P, ROW_PAIRS * PAIR], F32, name="nbr_acc")
-            for t in range(ROW_PAIRS):
-                pixels = nbr_acc[k][:, t * PAIR : (t + 1) * PAIR]
+        def transpose_patches(k):
+            b, part = divmod(k, CHUNKS_PER_IMAGE)
+            for h in range(BANKS_PER_CHUNK):
+                flipped[k, h] = psum_flip.tile([P, STRIPS, P], BF16, name="flipped")
+                first = part * CHUNK_ROWS + h * BANK_ROWS
+                for s in range(STRIPS):
+                    nc.tensor.transpose(
+                        flipped[k, h][:, s, :],
+                        strips[b][:, s, first : first + PATCH_ROWS, :].rearrange("p i j -> p (i j)"),
+                        ident[:],
+                    )
+
+        def sum_on_tensor_engine(k, h):
+            blocks = patches.tile([P, STRIPS, P], BF16, name="blocks")
+            nc.vector.tensor_copy(out=blocks[:], in_=flipped[k, h][:])
+            nbr_acc[k, h] = psum_nbr.tile([P, SIDE * TENSOR_ROWS], F32, name="nbr_acc")
+            for s in range(STRIPS):
+                lo = 0 if s == 0 else 1
+                hi = PATCH_COLS if s == STRIPS - 1 else STRIP_STEP + 1
                 nc.tensor.matmul(
-                    out=pixels,
-                    lhsT=blocks[:, t, :],
-                    rhs=from_upper[:].rearrange("p i j -> p (i j)"),
+                    out=nbr_acc[k, h][:, (s * STRIP_STEP + lo) * TENSOR_ROWS : (s * STRIP_STEP + hi) * TENSOR_ROWS],
+                    lhsT=blocks[:, s, :],
+                    rhs=window[:].rearrange("p j o -> p (j o)")[:, lo * TENSOR_ROWS : hi * TENSOR_ROWS],
                     start=True,
-                    stop=False,
-                )
-                nc.tensor.matmul(
-                    out=pixels,
-                    lhsT=blocks[:, t + 1, :],
-                    rhs=from_lower[:].rearrange("p i j -> p (i j)"),
-                    start=False,
                     stop=True,
                 )
-
-        def four_fold(k, first, values, count):
-            h, start = divmod(first, BANK)
-            if start == 0:
-                quad[k, h] = quads.tile([P, BANK * PACK], BF16, name="quad")
-            nc.scalar.copy(
-                out=quad[k, h][:, start * PACK : (start + count) * PACK].rearrange("p (w t) -> p w t", t=PACK),
-                in_=values.unsqueeze(2).to_broadcast([P, count, PACK]),
-            )
 
         def spread(k, h):
             xn[k, h] = moving.tile([P, PASSES * BANK * PACK], BF16, name="xn", align_bytes=64)
@@ -203,15 +205,24 @@ def tile_qca_operator_deep_pa_t_kernel(tc, x_cat, w1_words, w1_scales, out):
                     in_=quad[k, h][g::PASSES, :].unsqueeze(1).to_broadcast([PASS_CHANNELS, 2, BANK * PACK]),
                 )
 
-        def repeat_tensor_rows(k):
-            four_fold(k, 0, nbr_acc[k][:], TENSOR_PIXELS)
+        def repeat_tensor_rows(k, h):
+            quad[k, h] = quads.tile([P, BANK * PACK], BF16, name="quad")
+            nc.scalar.copy(
+                out=quad[k, h][:, 0 : TENSOR_PIXELS * PACK].rearrange("p (o j t) -> p o j t", o=TENSOR_ROWS, t=PACK),
+                in_=nbr_acc[k, h][:]
+                .rearrange("p (j o) -> p o j", o=TENSOR_ROWS)
+                .unsqueeze(3)
+                .to_broadcast([P, TENSOR_ROWS, SIDE, PACK]),
+            )
 
-        def repeat_vector_rows(k):
-            rest = BANK - TENSOR_PIXELS
-            four_fold(k, TENSOR_PIXELS, nbr[k][:, 0:rest], rest)
-            spread(k, 0)
-            four_fold(k, BANK, nbr[k][:, rest:VECTOR_PIXELS], BANK)
-            spread(k, 1)
+        def repeat_vector_rows(k, h):
+            nc.scalar.copy(
+                out=quad[k, h][:, TENSOR_PIXELS * PACK : BANK * PACK].rearrange("p (w t) -> p w t", t=PACK),
+                in_=nbr[k][:, h * VECTOR_PIXELS : (h + 1) * VECTOR_PIXELS]
+                .unsqueeze(2)
+                .to_broadcast([P, VECTOR_PIXELS, PACK]),
+            )
+            spread(k, h)
 
         def quantise_and_multiply(k, h):
             codes = packed.tile([P, PASSES * BANK], U32, name="codes", align_bytes=64)
@@ -248,7 +259,10 @@ def tile_qca_operator_deep_pa_t_kernel(tc, x_cat, w1_words, w1_scales, out):
             nc.sync.dma_start(out=out[b, :, first : first + bank_rows, :].rearrange("o i j -> o (i j)"), in_=res[:])
 
         with tc.manual_schedule():
-            transpose_rows(0)
+            half = SIDE // 2
+            for s in range(STRIPS):
+                copy_strip(0, s, 0, half)
+            transpose_patches(0)
             for j in range(N_CHUNKS + FINISH_LAG):
                 summing = j < N_CHUNKS
                 q = j - QUANTISE_LAG
@@ -266,8 +280,9 @@ def tile_qca_operator_deep_pa_t_kernel(tc, x_cat, w1_words, w1_scales, out):
                     exponentials(q)
                 if summing:
                     add_left_and_right(j)
-                    sum_on_tensor_engine(j)
-                    repeat_tensor_rows(j)
+                    for h in range(BANKS_PER_CHUNK):
+                        sum_on_tensor_engine(j, h)
+                        repeat_tensor_rows(j, h)
                 if quantising:
                     negative_part(q)
                 if finishing:
@@ -275,6 +290,15 @@ def tile_qca_operator_deep_pa_t_kernel(tc, x_cat, w1_words, w1_scales, out):
                     finish(f, 1)
                 if summing:
                     add_up_and_round(j)
-                    repeat_vector_rows(j)
+                    for h in range(BANKS_PER_CHUNK):
+                        repeat_vector_rows(j, h)
+                if j == 0:
+                    for s in range(STRIPS):
+                        copy_strip(0, s, half, half)
+                b, part = divmod(j, CHUNKS_PER_IMAGE)
+                if b + 1 < IMAGES:
+                    for s in range(STRIPS):
+                        if min(s, CHUNKS_PER_IMAGE - 1) == part:
+                            copy_strip(b + 1, s, 0, SIDE)
                 if j + 1 < N_CHUNKS:
-                    transpose_rows(j + 1)
+                    transpose_patches(j + 1)

@@ -14,9 +14,8 @@ FP8X4 = mybir.dt.float8_e4m3fn_x4
 FP4X4 = mybir.dt.float4_e2m1fn_x4
 ADD = mybir.AluOpType.add
 MAX = mybir.AluOpType.max
-SUBTRACT = mybir.AluOpType.subtract
+MIN = mybir.AluOpType.min
 EXP = mybir.ActivationFunctionType.Exp
-RELU = mybir.ActivationFunctionType.Relu
 
 P = 128
 PACK = 4
@@ -58,8 +57,7 @@ def tile_qca_operator_deep_pa_t_kernel(tc, x_cat, w1_words, w1_scales, out):
         nbrs = stack.enter_context(tc.tile_pool(name="nbrs", bufs=3))
         strip_pool = stack.enter_context(tc.tile_pool(name="strip_pool", bufs=2))
         patches = stack.enter_context(tc.tile_pool(name="patches", bufs=2 * BANKS_PER_CHUNK))
-        quads = stack.enter_context(tc.tile_pool(name="quads", bufs=2 * BANKS_PER_CHUNK))
-        moving = stack.enter_context(tc.tile_pool(name="moving", bufs=(QUANTISE_LAG + 1) * BANKS_PER_CHUNK))
+        moving = stack.enter_context(tc.tile_pool(name="moving", bufs=(QUANTISE_LAG + 2) * BANKS_PER_CHUNK))
         packed = stack.enter_context(tc.tile_pool(name="packed", bufs=3))
         tails = stack.enter_context(tc.tile_pool(name="tails", bufs=FINISH_LAG - QUANTISE_LAG + 1))
         results = stack.enter_context(tc.tile_pool(name="results", bufs=4))
@@ -125,7 +123,6 @@ def tile_qca_operator_deep_pa_t_kernel(tc, x_cat, w1_words, w1_scales, out):
         strips = {}
         flipped = {}
         nbr_acc = {}
-        quad = {}
         xn = {}
         acc = {}
         neg = {}
@@ -197,18 +194,19 @@ def tile_qca_operator_deep_pa_t_kernel(tc, x_cat, w1_words, w1_scales, out):
                     stop=True,
                 )
 
-        def spread(k, h):
-            xn[k, h] = moving.tile([P, PASSES * BANK * PACK], BF16, name="xn", align_bytes=64)
-            for g in range(PASSES):
-                nc.sync.dma_start(
-                    out=xn[k, h][:, g * BANK * PACK : (g + 1) * BANK * PACK],
-                    in_=quad[k, h][g::PASSES, :].unsqueeze(1).to_broadcast([PASS_CHANNELS, 2, BANK * PACK]),
-                )
+        def spread_second_pass(k, h):
+            nc.sync.dma_start(
+                out=xn[k, h][:, BANK * PACK : PASSES * BANK * PACK],
+                in_=xn[k, h][1::PASSES, 0 : BANK * PACK].unsqueeze(1).to_broadcast([PASS_CHANNELS, 2, BANK * PACK]),
+            )
+
+        def spread_first_pass(k, h):
+            nc.sync.dma_start(out=xn[k, h][1::PASSES, 0 : BANK * PACK], in_=xn[k, h][0::PASSES, 0 : BANK * PACK])
 
         def repeat_tensor_rows(k, h):
-            quad[k, h] = quads.tile([P, BANK * PACK], BF16, name="quad")
+            xn[k, h] = moving.tile([P, PASSES * BANK * PACK], BF16, name="xn", align_bytes=64)
             nc.scalar.copy(
-                out=quad[k, h][:, 0 : TENSOR_PIXELS * PACK].rearrange("p (o j t) -> p o j t", o=TENSOR_ROWS, t=PACK),
+                out=xn[k, h][:, 0 : TENSOR_PIXELS * PACK].rearrange("p (o j t) -> p o j t", o=TENSOR_ROWS, t=PACK),
                 in_=nbr_acc[k, h][:]
                 .rearrange("p (j o) -> p o j", o=TENSOR_ROWS)
                 .unsqueeze(3)
@@ -217,12 +215,12 @@ def tile_qca_operator_deep_pa_t_kernel(tc, x_cat, w1_words, w1_scales, out):
 
         def repeat_vector_rows(k, h):
             nc.scalar.copy(
-                out=quad[k, h][:, TENSOR_PIXELS * PACK : BANK * PACK].rearrange("p (w t) -> p w t", t=PACK),
+                out=xn[k, h][:, TENSOR_PIXELS * PACK : BANK * PACK].rearrange("p (w t) -> p w t", t=PACK),
                 in_=nbr[k][:, h * VECTOR_PIXELS : (h + 1) * VECTOR_PIXELS]
                 .unsqueeze(2)
                 .to_broadcast([P, VECTOR_PIXELS, PACK]),
             )
-            spread(k, h)
+            spread_second_pass(k, h)
 
         def quantise_and_multiply(k, h):
             codes = packed.tile([P, PASSES * BANK], U32, name="codes", align_bytes=64)
@@ -246,13 +244,11 @@ def tile_qca_operator_deep_pa_t_kernel(tc, x_cat, w1_words, w1_scales, out):
                 nc.scalar.activation(out=neg[k][:, h * BANK : (h + 1) * BANK], in_=acc[k, h][:], func=EXP)
 
         def negative_part(k):
-            nc.scalar.activation(out=neg[k][:], in_=neg[k][:], func=RELU, bias=1.0, scale=-1.0)
+            nc.vector.tensor_scalar(out=neg[k][:], in0=neg[k][:], scalar1=1.0, scalar2=-1.0, op0=MIN, op1=ADD)
 
         def finish(k, h):
             res = results.tile([HID, BANK], F32, name="res")
-            nc.vector.scalar_tensor_tensor(
-                out=res[:], in0=acc[k, h][:], scalar=0.0, in1=neg[k][:, h * BANK : (h + 1) * BANK], op0=MAX, op1=SUBTRACT
-            )
+            nc.vector.tensor_tensor(out=res[:], in0=acc[k, h][:], in1=neg[k][:, h * BANK : (h + 1) * BANK], op=MAX)
             b, part = divmod(k, CHUNKS_PER_IMAGE)
             bank_rows = BANK // SIDE
             first = part * CHUNK_ROWS + h * bank_rows
@@ -273,6 +269,8 @@ def tile_qca_operator_deep_pa_t_kernel(tc, x_cat, w1_words, w1_scales, out):
                     add_above_and_below(j)
                 if quantising:
                     quantise_and_multiply(q, 0)
+                if finishing:
+                    negative_part(f)
                 if summing:
                     add_centre(j)
                 if quantising:
@@ -283,8 +281,6 @@ def tile_qca_operator_deep_pa_t_kernel(tc, x_cat, w1_words, w1_scales, out):
                     for h in range(BANKS_PER_CHUNK):
                         sum_on_tensor_engine(j, h)
                         repeat_tensor_rows(j, h)
-                if quantising:
-                    negative_part(q)
                 if finishing:
                     finish(f, 0)
                     finish(f, 1)
@@ -292,6 +288,8 @@ def tile_qca_operator_deep_pa_t_kernel(tc, x_cat, w1_words, w1_scales, out):
                     add_up_and_round(j)
                     for h in range(BANKS_PER_CHUNK):
                         repeat_vector_rows(j, h)
+                    for h in range(BANKS_PER_CHUNK):
+                        spread_first_pass(j, h)
                 if j == 0:
                     for s in range(STRIPS):
                         copy_strip(0, s, half, half)

@@ -15,7 +15,9 @@ FP4X4 = mybir.dt.float4_e2m1fn_x4
 ADD = mybir.AluOpType.add
 MAX = mybir.AluOpType.max
 MIN = mybir.AluOpType.min
+MULT = mybir.AluOpType.mult
 EXP = mybir.ActivationFunctionType.Exp
+RELU = mybir.ActivationFunctionType.Relu
 
 P = 128
 PACK = 4
@@ -45,8 +47,8 @@ VECTOR_PIXELS = VECTOR_ROWS * SIDE
 TENSOR_PIXELS = TENSOR_ROWS * SIDE
 PAD_ROWS = SIDE + BANK_ROWS
 
-QUANTISE_LAG = 3
-FINISH_LAG = 4
+QUANTISE_LAG = 4
+FINISH_LAG = 5
 
 
 def tile_qca_operator_deep_pa_t_kernel(tc, x_cat, w1_words, w1_scales, out):
@@ -54,13 +56,13 @@ def tile_qca_operator_deep_pa_t_kernel(tc, x_cat, w1_words, w1_scales, out):
     with ExitStack() as stack:
         keep = stack.enter_context(tc.tile_pool(name="keep", bufs=1))
         sums = stack.enter_context(tc.tile_pool(name="sums", bufs=2))
-        nbrs = stack.enter_context(tc.tile_pool(name="nbrs", bufs=3))
+        nbrs = stack.enter_context(tc.tile_pool(name="nbrs", bufs=QUANTISE_LAG + 3))
         strip_pool = stack.enter_context(tc.tile_pool(name="strip_pool", bufs=2))
         patches = stack.enter_context(tc.tile_pool(name="patches", bufs=2 * BANKS_PER_CHUNK))
         moving = stack.enter_context(tc.tile_pool(name="moving", bufs=(QUANTISE_LAG + 2) * BANKS_PER_CHUNK))
         packed = stack.enter_context(tc.tile_pool(name="packed", bufs=3))
         tails = stack.enter_context(tc.tile_pool(name="tails", bufs=FINISH_LAG - QUANTISE_LAG + 1))
-        results = stack.enter_context(tc.tile_pool(name="results", bufs=4))
+        results = stack.enter_context(tc.tile_pool(name="results", bufs=8))
         psum_flip = stack.enter_context(tc.psum_pool(name="psum_flip", bufs=BANKS_PER_CHUNK))
         psum_nbr = stack.enter_context(tc.psum_pool(name="psum_nbr", bufs=BANKS_PER_CHUNK))
         psum_acc = stack.enter_context(tc.psum_pool(name="psum_acc", bufs=2 * BANKS_PER_CHUNK))
@@ -82,7 +84,8 @@ def tile_qca_operator_deep_pa_t_kernel(tc, x_cat, w1_words, w1_scales, out):
                     ),
                 )
 
-        load_rows(0, 0, CHUNK_ROWS)
+        for part in range(CHUNKS_PER_IMAGE):
+            load_rows(0, part * CHUNK_ROWS, CHUNK_ROWS)
         for g in range(PASSES):
             nc.sync.dma_start(out=w_codes[:, g, :].bitcast(I32), in_=w1_words[g].bitcast(I32))
             for quadrant in range(4):
@@ -90,8 +93,6 @@ def tile_qca_operator_deep_pa_t_kernel(tc, x_cat, w1_words, w1_scales, out):
                     out=w_planes[32 * quadrant : 32 * quadrant + 4, g, :].bitcast(I32),
                     in_=w1_scales[g, 4 * quadrant : 4 * quadrant + 4, :].bitcast(I32),
                 )
-        for part in range(1, CHUNKS_PER_IMAGE):
-            load_rows(0, part * CHUNK_ROWS, CHUNK_ROWS)
         for b in range(1, IMAGES):
             load_rows(b, 0, SIDE)
 
@@ -214,7 +215,8 @@ def tile_qca_operator_deep_pa_t_kernel(tc, x_cat, w1_words, w1_scales, out):
             )
 
         def repeat_vector_rows(k, h):
-            nc.scalar.copy(
+            copy = nc.vector.tensor_copy if k < QUANTISE_LAG else nc.scalar.copy
+            copy(
                 out=xn[k, h][:, TENSOR_PIXELS * PACK : BANK * PACK].rearrange("p (w t) -> p w t", t=PACK),
                 in_=nbr[k][:, h * VECTOR_PIXELS : (h + 1) * VECTOR_PIXELS]
                 .unsqueeze(2)
@@ -238,61 +240,91 @@ def tile_qca_operator_deep_pa_t_kernel(tc, x_cat, w1_words, w1_scales, out):
                     stop=(g == PASSES - 1),
                 )
 
+        def scalar_takes(k, h):
+            return k >= N_CHUNKS - QUANTISE_LAG
+
         def exponentials(k):
             neg[k] = tails.tile([HID, CHUNK], F32, name="neg")
             for h in range(BANKS_PER_CHUNK):
                 nc.scalar.activation(out=neg[k][:, h * BANK : (h + 1) * BANK], in_=acc[k, h][:], func=EXP)
 
-        def negative_part(k):
-            nc.vector.tensor_scalar(out=neg[k][:], in0=neg[k][:], scalar1=1.0, scalar2=-1.0, op0=MIN, op1=ADD)
+        def negative_part(k, on_scalar):
+            for h in range(BANKS_PER_CHUNK):
+                part = neg[k][:, h * BANK : (h + 1) * BANK]
+                if on_scalar and scalar_takes(k, h):
+                    nc.scalar.activation(out=part, in_=part, func=RELU, bias=1.0, scale=-1.0)
+                if not on_scalar and not scalar_takes(k, h):
+                    nc.vector.tensor_scalar(out=part, in0=part, scalar1=1.0, scalar2=-1.0, op0=MIN, op1=ADD)
 
         def finish(k, h):
             res = results.tile([HID, BANK], F32, name="res")
-            nc.vector.tensor_tensor(out=res[:], in0=acc[k, h][:], in1=neg[k][:, h * BANK : (h + 1) * BANK], op=MAX)
+            nc.vector.scalar_tensor_tensor(
+                out=res[:],
+                in0=neg[k][:, h * BANK : (h + 1) * BANK],
+                scalar=-1.0 if scalar_takes(k, h) else 1.0,
+                in1=acc[k, h][:],
+                op0=MULT,
+                op1=MAX,
+            )
             b, part = divmod(k, CHUNKS_PER_IMAGE)
             bank_rows = BANK // SIDE
             first = part * CHUNK_ROWS + h * bank_rows
             nc.sync.dma_start(out=out[b, :, first : first + bank_rows, :].rearrange("o i j -> o (i j)"), in_=res[:])
 
+        def chunks_to_sum(j):
+            if j < QUANTISE_LAG:
+                return [2 * j, 2 * j + 1]
+            return [k for k in [j + QUANTISE_LAG] if k < N_CHUNKS]
+
         with tc.manual_schedule():
-            half = SIDE // 2
             for s in range(STRIPS):
-                copy_strip(0, s, 0, half)
+                copy_strip(0, s, 0, CHUNK_ROWS)
             transpose_patches(0)
             for j in range(N_CHUNKS + FINISH_LAG):
-                summing = j < N_CHUNKS
+                repeating = j < N_CHUNKS
                 q = j - QUANTISE_LAG
                 quantising = 0 <= q < N_CHUNKS
                 f = j - FINISH_LAG
                 finishing = 0 <= f
-                if summing:
-                    add_above_and_below(j)
+                summed = chunks_to_sum(j)
+                for k in summed:
+                    add_above_and_below(k)
                 if quantising:
                     quantise_and_multiply(q, 0)
                 if finishing:
-                    negative_part(f)
-                if summing:
-                    add_centre(j)
+                    negative_part(f, False)
+                for k in summed[0:1]:
+                    add_centre(k)
                 if quantising:
                     quantise_and_multiply(q, 1)
                     exponentials(q)
-                if summing:
-                    add_left_and_right(j)
+                    negative_part(q, True)
+                for k in summed[0:1]:
+                    add_left_and_right(k)
+                if repeating:
                     for h in range(BANKS_PER_CHUNK):
                         sum_on_tensor_engine(j, h)
                         repeat_tensor_rows(j, h)
                 if finishing:
                     finish(f, 0)
                     finish(f, 1)
-                if summing:
-                    add_up_and_round(j)
-                    for h in range(BANKS_PER_CHUNK):
-                        repeat_vector_rows(j, h)
+                for k in summed[0:1]:
+                    add_up_and_round(k)
+                for k in summed[1:2]:
+                    add_centre(k)
+                if repeating:
+                    repeat_vector_rows(j, 0)
+                for k in summed[1:2]:
+                    add_left_and_right(k)
+                if repeating:
+                    repeat_vector_rows(j, 1)
                     for h in range(BANKS_PER_CHUNK):
                         spread_first_pass(j, h)
+                for k in summed[1:2]:
+                    add_up_and_round(k)
                 if j == 0:
                     for s in range(STRIPS):
-                        copy_strip(0, s, half, half)
+                        copy_strip(0, s, CHUNK_ROWS, SIDE - CHUNK_ROWS)
                 b, part = divmod(j, CHUNKS_PER_IMAGE)
                 if b + 1 < IMAGES:
                     for s in range(STRIPS):

@@ -42,7 +42,7 @@ TENSOR_ROWS = PATCH_ROWS - 2
 STRIPS = 5
 STRIP_STEP = 12
 VECTOR_ROWS = BANK_ROWS - TENSOR_ROWS
-CHUNK_VECTOR_ROWS = VECTOR_ROWS * BANKS_PER_CHUNK
+BANKS_PER_IMAGE = SIDE // BANK_ROWS
 VECTOR_PIXELS = VECTOR_ROWS * SIDE
 TENSOR_PIXELS = TENSOR_ROWS * SIDE
 PAD_ROWS = SIDE + BANK_ROWS
@@ -56,7 +56,7 @@ def tile_qca_operator_deep_pa_t_kernel(tc, x_cat, w1_words, w1_scales, out):
     with ExitStack() as stack:
         keep = stack.enter_context(tc.tile_pool(name="keep", bufs=1))
         sums = stack.enter_context(tc.tile_pool(name="sums", bufs=2))
-        nbrs = stack.enter_context(tc.tile_pool(name="nbrs", bufs=QUANTISE_LAG + 3))
+        nbrs = stack.enter_context(tc.tile_pool(name="nbrs", bufs=5))
         strip_pool = stack.enter_context(tc.tile_pool(name="strip_pool", bufs=2))
         patches = stack.enter_context(tc.tile_pool(name="patches", bufs=2 * BANKS_PER_CHUNK))
         moving = stack.enter_context(tc.tile_pool(name="moving", bufs=(QUANTISE_LAG + 2) * BANKS_PER_CHUNK))
@@ -69,8 +69,10 @@ def tile_qca_operator_deep_pa_t_kernel(tc, x_cat, w1_words, w1_scales, out):
 
         x_pad = keep.tile([P, IMAGES, PAD_ROWS, SIDE], BF16, name="x_pad")
         nc.vector.memset(x_pad[:, :, 0 : SIDE + 2 : SIDE + 1, :], 0.0)
-        col_sum = keep.tile([P, CHUNK_VECTOR_ROWS * PITCH + 2], F32, name="col_sum")
-        nc.vector.memset(col_sum[:], 0.0)
+        col_sum = {}
+        for banks in (BANKS_PER_CHUNK, BANKS_PER_IMAGE):
+            col_sum[banks] = keep.tile([P, banks * VECTOR_ROWS * PITCH + 2], F32, name="col_sum%d" % banks)
+            nc.vector.memset(col_sum[banks][:], 0.0)
         w_codes = keep.tile([P, PASSES, 2 * HID], U8, name="w_codes", align_bytes=64)
         w_planes = keep.tile([P, PASSES, HID], U8, name="w_planes", align_bytes=64)
         nc.vector.memset(w_planes[:].rearrange("p g n -> p (g n)").bitcast(I32), 0)
@@ -129,36 +131,46 @@ def tile_qca_operator_deep_pa_t_kernel(tc, x_cat, w1_words, w1_scales, out):
         neg = {}
 
         def rows_of(flat):
-            return flat.rearrange("p (h r j) -> p h r j", h=BANKS_PER_CHUNK, j=SIDE)
+            return flat.rearrange("p (g r j) -> p g r j", r=VECTOR_ROWS, j=SIDE)
 
-        def column_sums(first):
-            return col_sum[:, first : first + CHUNK_VECTOR_ROWS * PITCH].rearrange(
-                "p (h r j) -> p h r j", h=BANKS_PER_CHUNK, j=PITCH
+        def column_sums(batch, shift):
+            banks = batch[2]
+            return col_sum[banks][:, shift : shift + banks * VECTOR_ROWS * PITCH].rearrange(
+                "p (g r j) -> p g r j", r=VECTOR_ROWS, j=PITCH
             )[:, :, :, 0:SIDE]
 
-        def padded_rows(k, offset):
-            b, part = divmod(k, CHUNKS_PER_IMAGE)
-            first = part * CHUNK_ROWS + TENSOR_ROWS + offset
-            return x_pad[:, b, first : first + CHUNK_ROWS, :].rearrange("p (h r) j -> p h r j", r=BANK_ROWS)[
+        def padded_rows(batch, offset):
+            b, first, banks = batch
+            top = first * BANK_ROWS + TENSOR_ROWS + offset
+            return x_pad[:, b, top : top + banks * BANK_ROWS, :].rearrange("p (g r) j -> p g r j", r=BANK_ROWS)[
                 :, :, 0:VECTOR_ROWS, :
             ]
 
-        def add_above_and_below(k):
-            above_below[k] = sums.tile([P, CHUNK_VECTOR_ROWS * SIDE], F32, name="above_below")
+        def add_above_and_below(batch):
+            above_below[batch] = sums.tile([P, batch[2] * VECTOR_PIXELS], F32, name="above_below")
             nc.vector.tensor_tensor(
-                out=rows_of(above_below[k][:]), in0=padded_rows(k, 0), in1=padded_rows(k, 2), op=ADD
+                out=rows_of(above_below[batch][:]), in0=padded_rows(batch, 0), in1=padded_rows(batch, 2), op=ADD
             )
 
-        def add_centre(k):
-            nc.vector.tensor_tensor(out=column_sums(1), in0=rows_of(above_below[k][:]), in1=padded_rows(k, 1), op=ADD)
+        def add_centre(batch):
+            nc.vector.tensor_tensor(
+                out=column_sums(batch, 1), in0=rows_of(above_below[batch][:]), in1=padded_rows(batch, 1), op=ADD
+            )
 
-        def add_left_and_right(k):
-            left_right[k] = sums.tile([P, CHUNK_VECTOR_ROWS * SIDE], F32, name="left_right")
-            nc.vector.tensor_tensor(out=rows_of(left_right[k][:]), in0=column_sums(0), in1=column_sums(2), op=ADD)
+        def add_left_and_right(batch):
+            left_right[batch] = sums.tile([P, batch[2] * VECTOR_PIXELS], F32, name="left_right")
+            nc.vector.tensor_tensor(
+                out=rows_of(left_right[batch][:]), in0=column_sums(batch, 0), in1=column_sums(batch, 2), op=ADD
+            )
 
-        def add_up_and_round(k):
-            nbr[k] = nbrs.tile([P, CHUNK_VECTOR_ROWS * SIDE], BF16, name="nbr")
-            nc.vector.tensor_tensor(out=nbr[k][:], in0=left_right[k][:], in1=above_below[k][:], op=ADD)
+        def add_up_and_round(batch):
+            b, first, banks = batch
+            rounded = nbrs.tile([P, banks * VECTOR_PIXELS], BF16, name="rounded")
+            nc.vector.tensor_tensor(out=rounded[:], in0=left_right[batch][:], in1=above_below[batch][:], op=ADD)
+            for g in range(banks):
+                nbr[b, first + g] = rounded[:, g * VECTOR_PIXELS : (g + 1) * VECTOR_PIXELS]
+
+        add_steps = [add_above_and_below, add_centre, add_left_and_right, add_up_and_round]
 
         def copy_strip(b, s, first, count):
             if b not in strips:
@@ -218,7 +230,7 @@ def tile_qca_operator_deep_pa_t_kernel(tc, x_cat, w1_words, w1_scales, out):
             copy = nc.vector.tensor_copy if k < QUANTISE_LAG else nc.scalar.copy
             copy(
                 out=xn[k, h][:, TENSOR_PIXELS * PACK : BANK * PACK].rearrange("p (w t) -> p w t", t=PACK),
-                in_=nbr[k][:, h * VECTOR_PIXELS : (h + 1) * VECTOR_PIXELS]
+                in_=nbr[k // CHUNKS_PER_IMAGE, (k % CHUNKS_PER_IMAGE) * BANKS_PER_CHUNK + h]
                 .unsqueeze(2)
                 .to_broadcast([P, VECTOR_PIXELS, PACK]),
             )
@@ -249,12 +261,14 @@ def tile_qca_operator_deep_pa_t_kernel(tc, x_cat, w1_words, w1_scales, out):
                 nc.scalar.activation(out=neg[k][:, h * BANK : (h + 1) * BANK], in_=acc[k, h][:], func=EXP)
 
         def negative_part(k, on_scalar):
-            for h in range(BANKS_PER_CHUNK):
-                part = neg[k][:, h * BANK : (h + 1) * BANK]
-                if on_scalar and scalar_takes(k, h):
+            mine = [h for h in range(BANKS_PER_CHUNK) if scalar_takes(k, h) == on_scalar]
+            if on_scalar:
+                for h in mine:
+                    part = neg[k][:, h * BANK : (h + 1) * BANK]
                     nc.scalar.activation(out=part, in_=part, func=RELU, bias=1.0, scale=-1.0)
-                if not on_scalar and not scalar_takes(k, h):
-                    nc.vector.tensor_scalar(out=part, in0=part, scalar1=1.0, scalar2=-1.0, op0=MIN, op1=ADD)
+            elif mine:
+                part = neg[k][:, mine[0] * BANK : (mine[-1] + 1) * BANK]
+                nc.vector.tensor_scalar(out=part, in0=part, scalar1=1.0, scalar2=-1.0, op0=MIN, op1=ADD)
 
         def finish(k, h):
             res = results.tile([HID, BANK], F32, name="res")
@@ -271,10 +285,19 @@ def tile_qca_operator_deep_pa_t_kernel(tc, x_cat, w1_words, w1_scales, out):
             first = part * CHUNK_ROWS + h * bank_rows
             nc.sync.dma_start(out=out[b, :, first : first + bank_rows, :].rearrange("o i j -> o (i j)"), in_=res[:])
 
-        def chunks_to_sum(j):
-            if j < QUANTISE_LAG:
-                return [2 * j, 2 * j + 1]
-            return [k for k in [j + QUANTISE_LAG] if k < N_CHUNKS]
+        def whole_sums(j):
+            if j < 2:
+                return [(0, (2 * j + i) * BANKS_PER_CHUNK, BANKS_PER_CHUNK) for i in range(2)]
+            return []
+
+        def single_adds(j):
+            if j in (2, 3):
+                first = 2 * (j - 2)
+                return [(0, (add_steps[first], (1, 0, BANKS_PER_IMAGE))), (2, (add_steps[first + 1], (1, 0, BANKS_PER_IMAGE)))]
+            b, stage = divmod(j + CHUNKS_PER_IMAGE, CHUNKS_PER_IMAGE)
+            if 2 <= b < IMAGES:
+                return [(1, (add_steps[stage], (b, 0, BANKS_PER_IMAGE)))]
+            return []
 
         with tc.manual_schedule():
             for s in range(STRIPS):
@@ -286,21 +309,28 @@ def tile_qca_operator_deep_pa_t_kernel(tc, x_cat, w1_words, w1_scales, out):
                 quantising = 0 <= q < N_CHUNKS
                 f = j - FINISH_LAG
                 finishing = 0 <= f
-                summed = chunks_to_sum(j)
-                for k in summed:
-                    add_above_and_below(k)
+                summed = whole_sums(j)
+                singles = single_adds(j)
+                for batch in summed:
+                    add_above_and_below(batch)
+                for place, (step, batch) in singles:
+                    if place == 0:
+                        step(batch)
                 if quantising:
                     quantise_and_multiply(q, 0)
                 if finishing:
                     negative_part(f, False)
-                for k in summed[0:1]:
-                    add_centre(k)
+                for batch in summed[0:1]:
+                    add_centre(batch)
+                for place, (step, batch) in singles:
+                    if place == 1:
+                        step(batch)
                 if quantising:
                     quantise_and_multiply(q, 1)
                     exponentials(q)
                     negative_part(q, True)
-                for k in summed[0:1]:
-                    add_left_and_right(k)
+                for batch in summed[0:1]:
+                    add_left_and_right(batch)
                 if repeating:
                     for h in range(BANKS_PER_CHUNK):
                         sum_on_tensor_engine(j, h)
@@ -308,20 +338,23 @@ def tile_qca_operator_deep_pa_t_kernel(tc, x_cat, w1_words, w1_scales, out):
                 if finishing:
                     finish(f, 0)
                     finish(f, 1)
-                for k in summed[0:1]:
-                    add_up_and_round(k)
-                for k in summed[1:2]:
-                    add_centre(k)
+                for batch in summed[0:1]:
+                    add_up_and_round(batch)
+                for batch in summed[1:2]:
+                    add_centre(batch)
+                for place, (step, batch) in singles:
+                    if place == 2:
+                        step(batch)
                 if repeating:
                     repeat_vector_rows(j, 0)
-                for k in summed[1:2]:
-                    add_left_and_right(k)
+                for batch in summed[1:2]:
+                    add_left_and_right(batch)
                 if repeating:
                     repeat_vector_rows(j, 1)
                     for h in range(BANKS_PER_CHUNK):
                         spread_first_pass(j, h)
-                for k in summed[1:2]:
-                    add_up_and_round(k)
+                for batch in summed[1:2]:
+                    add_up_and_round(batch)
                 if j == 0:
                     for s in range(STRIPS):
                         copy_strip(0, s, CHUNK_ROWS, SIDE - CHUNK_ROWS)

@@ -115,10 +115,8 @@ def tile_qca_operator_deep_pa_t_kernel(tc, x_cat, w1_words, w1_scales, out):
         nc.vector.tensor_tensor(
             out=outer[:], in0=around[:, 0:TENSOR_ROWS, :], in1=around[:, 2 : TENSOR_ROWS + 2, :], op=ADD
         )
-        window = keep.tile([P, PATCH_COLS, TENSOR_ROWS], BF16, name="window")
-        nc.vector.tensor_tensor(
-            out=window[:].rearrange("p j o -> p o j"), in0=outer[:], in1=beside[:, 1 : TENSOR_ROWS + 1, :], op=ADD
-        )
+        window = keep.tile([P, TENSOR_ROWS, PATCH_COLS], BF16, name="window")
+        nc.vector.tensor_tensor(out=window[:], in0=outer[:], in1=beside[:, 1 : TENSOR_ROWS + 1, :], op=ADD)
 
         above_below = {}
         left_right = {}
@@ -195,14 +193,14 @@ def tile_qca_operator_deep_pa_t_kernel(tc, x_cat, w1_words, w1_scales, out):
         def sum_on_tensor_engine(k, h):
             blocks = patches.tile([P, STRIPS, P], BF16, name="blocks")
             nc.vector.tensor_copy(out=blocks[:], in_=flipped[k, h][:])
-            nbr_acc[k, h] = psum_nbr.tile([P, SIDE * TENSOR_ROWS], F32, name="nbr_acc")
+            nbr_acc[k, h] = psum_nbr.tile([P, TENSOR_ROWS, SIDE], F32, name="nbr_acc")
             for s in range(STRIPS):
                 lo = 0 if s == 0 else 1
                 hi = PATCH_COLS if s == STRIPS - 1 else STRIP_STEP + 1
                 nc.tensor.matmul(
-                    out=nbr_acc[k, h][:, (s * STRIP_STEP + lo) * TENSOR_ROWS : (s * STRIP_STEP + hi) * TENSOR_ROWS],
+                    out=nbr_acc[k, h][:, :, s * STRIP_STEP + lo : s * STRIP_STEP + hi],
                     lhsT=blocks[:, s, :],
-                    rhs=window[:].rearrange("p j o -> p (j o)")[:, lo * TENSOR_ROWS : hi * TENSOR_ROWS],
+                    rhs=window[:, :, lo:hi],
                     start=True,
                     stop=True,
                 )
@@ -219,11 +217,11 @@ def tile_qca_operator_deep_pa_t_kernel(tc, x_cat, w1_words, w1_scales, out):
         def repeat_tensor_rows(k, h):
             xn[k, h] = moving.tile([P, PASSES * BANK * PACK], BF16, name="xn", align_bytes=64)
             nc.scalar.copy(
-                out=xn[k, h][:, 0 : TENSOR_PIXELS * PACK].rearrange("p (o j t) -> p o j t", o=TENSOR_ROWS, t=PACK),
+                out=xn[k, h][:, 0 : TENSOR_PIXELS * PACK].rearrange("p (w t) -> p w t", t=PACK),
                 in_=nbr_acc[k, h][:]
-                .rearrange("p (j o) -> p o j", o=TENSOR_ROWS)
-                .unsqueeze(3)
-                .to_broadcast([P, TENSOR_ROWS, SIDE, PACK]),
+                .rearrange("p o j -> p (o j)")
+                .unsqueeze(2)
+                .to_broadcast([P, TENSOR_PIXELS, PACK]),
             )
 
         def repeat_vector_rows(k, h):

from contextlib import ExitStack

import concourse.mybir as mybir
from concourse.masks import make_identity

FLOPS = 2 * 4 * 64 * 64 * 1024 * 128

BF16 = mybir.dt.bfloat16
F32 = mybir.dt.float32
I32 = mybir.dt.int32
U32 = mybir.dt.uint32
U8 = mybir.dt.uint8
FP8X4 = mybir.dt.float8_e4m3fn_x4
FP4X4 = mybir.dt.float4_e2m1fn_x4
ADD = mybir.AluOpType.add
MAX = mybir.AluOpType.max
MIN = mybir.AluOpType.min
MULT = mybir.AluOpType.mult
EXP = mybir.ActivationFunctionType.Exp
RELU = mybir.ActivationFunctionType.Relu

P = 128
PACK = 4
IMAGES = 4
SIDE = 64
PASSES = 2
PASS_CHANNELS = 64
HID = 128

CHUNK_ROWS = 16
CHUNK = CHUNK_ROWS * SIDE
CHUNKS_PER_IMAGE = SIDE // CHUNK_ROWS
N_CHUNKS = IMAGES * CHUNKS_PER_IMAGE
BANK = 512
BANKS_PER_CHUNK = CHUNK // BANK
PITCH = SIDE + 1
BANK_ROWS = BANK // SIDE

PATCH_ROWS = 8
PATCH_COLS = 16
TENSOR_ROWS = PATCH_ROWS - 2
STRIPS = 5
STRIP_STEP = 12
VECTOR_ROWS = BANK_ROWS - TENSOR_ROWS
BANKS_PER_IMAGE = SIDE // BANK_ROWS
VECTOR_PIXELS = VECTOR_ROWS * SIDE
TENSOR_PIXELS = TENSOR_ROWS * SIDE
PAD_ROWS = SIDE + BANK_ROWS

QUANTISE_LAG = 4
FINISH_LAG = 5


def tile_qca_operator_deep_pa_t_kernel(tc, x_cat, w1_words, w1_scales, out):
    nc = tc.nc
    with ExitStack() as stack:
        keep = stack.enter_context(tc.tile_pool(name="keep", bufs=1))
        sums = stack.enter_context(tc.tile_pool(name="sums", bufs=2))
        nbrs = stack.enter_context(tc.tile_pool(name="nbrs", bufs=5))
        strip_pool = stack.enter_context(tc.tile_pool(name="strip_pool", bufs=2))
        patches = stack.enter_context(tc.tile_pool(name="patches", bufs=2 * BANKS_PER_CHUNK))
        moving = stack.enter_context(tc.tile_pool(name="moving", bufs=(QUANTISE_LAG + 2) * BANKS_PER_CHUNK))
        packed = stack.enter_context(tc.tile_pool(name="packed", bufs=3))
        tails = stack.enter_context(tc.tile_pool(name="tails", bufs=FINISH_LAG - QUANTISE_LAG + 1))
        results = stack.enter_context(tc.tile_pool(name="results", bufs=8))
        psum_flip = stack.enter_context(tc.psum_pool(name="psum_flip", bufs=BANKS_PER_CHUNK))
        psum_nbr = stack.enter_context(tc.psum_pool(name="psum_nbr", bufs=BANKS_PER_CHUNK))
        psum_acc = stack.enter_context(tc.psum_pool(name="psum_acc", bufs=2 * BANKS_PER_CHUNK))

        x_pad = keep.tile([P, IMAGES, PAD_ROWS, SIDE], BF16, name="x_pad")
        nc.vector.memset(x_pad[:, :, 0 : SIDE + 2 : SIDE + 1, :], 0.0)
        col_sum = {}
        for banks in (BANKS_PER_CHUNK, BANKS_PER_IMAGE):
            col_sum[banks] = keep.tile([P, banks * VECTOR_ROWS * PITCH + 2], F32, name="col_sum%d" % banks)
            nc.vector.memset(col_sum[banks][:], 0.0)
        w_codes = keep.tile([P, PASSES, 2 * HID], U8, name="w_codes", align_bytes=64)
        w_planes = keep.tile([P, PASSES, HID], U8, name="w_planes", align_bytes=64)
        nc.vector.memset(w_planes[:].rearrange("p g n -> p (g n)").bitcast(I32), 0)

        def load_rows(b, first, count):
            for g in range(PASSES):
                nc.sync.dma_start(
                    out=x_pad[g::PASSES, b, 1 + first : 1 + first + count, :].rearrange("c i j -> c (i j)"),
                    in_=x_cat[b, g * PASS_CHANNELS : (g + 1) * PASS_CHANNELS, first : first + count, :].rearrange(
                        "c i j -> c (i j)"
                    ),
                )

        for part in range(CHUNKS_PER_IMAGE):
            load_rows(0, part * CHUNK_ROWS, CHUNK_ROWS)
        for g in range(PASSES):
            nc.sync.dma_start(out=w_codes[:, g, :].bitcast(I32), in_=w1_words[g].bitcast(I32))
            for quadrant in range(4):
                nc.sync.dma_start(
                    out=w_planes[32 * quadrant : 32 * quadrant + 4, g, :].bitcast(I32),
                    in_=w1_scales[g, 4 * quadrant : 4 * quadrant + 4, :].bitcast(I32),
                )
        for b in range(1, IMAGES):
            load_rows(b, 0, SIDE)

        ident = keep.tile([P, P], BF16, name="ident")
        make_identity(nc, ident[:])
        ident_pad = keep.tile([P, PATCH_ROWS, PATCH_COLS + 2], BF16, name="ident_pad")
        nc.vector.memset(ident_pad[:], 0.0)
        nc.vector.tensor_copy(
            out=ident_pad[:, :, 1 : PATCH_COLS + 1], in_=ident[:].rearrange("p (i j) -> p i j", j=PATCH_COLS)
        )
        beside = keep.tile([P, PATCH_ROWS, PATCH_COLS], BF16, name="beside")
        nc.vector.tensor_tensor(
            out=beside[:], in0=ident_pad[:, :, 0:PATCH_COLS], in1=ident_pad[:, :, 2 : PATCH_COLS + 2], op=ADD
        )
        around = keep.tile([P, PATCH_ROWS, PATCH_COLS], BF16, name="around")
        nc.vector.tensor_tensor(out=around[:], in0=beside[:], in1=ident_pad[:, :, 1 : PATCH_COLS + 1], op=ADD)
        outer = keep.tile([P, TENSOR_ROWS, PATCH_COLS], BF16, name="outer")
        nc.vector.tensor_tensor(
            out=outer[:], in0=around[:, 0:TENSOR_ROWS, :], in1=around[:, 2 : TENSOR_ROWS + 2, :], op=ADD
        )
        window = keep.tile([P, TENSOR_ROWS, PATCH_COLS], BF16, name="window")
        nc.vector.tensor_tensor(out=window[:], in0=outer[:], in1=beside[:, 1 : TENSOR_ROWS + 1, :], op=ADD)

        above_below = {}
        left_right = {}
        nbr = {}
        strips = {}
        flipped = {}
        nbr_acc = {}
        xn = {}
        acc = {}
        neg = {}

        def rows_of(flat):
            return flat.rearrange("p (g r j) -> p g r j", r=VECTOR_ROWS, j=SIDE)

        def column_sums(batch, shift):
            banks = batch[2]
            return col_sum[banks][:, shift : shift + banks * VECTOR_ROWS * PITCH].rearrange(
                "p (g r j) -> p g r j", r=VECTOR_ROWS, j=PITCH
            )[:, :, :, 0:SIDE]

        def padded_rows(batch, offset):
            b, first, banks = batch
            top = first * BANK_ROWS + TENSOR_ROWS + offset
            return x_pad[:, b, top : top + banks * BANK_ROWS, :].rearrange("p (g r) j -> p g r j", r=BANK_ROWS)[
                :, :, 0:VECTOR_ROWS, :
            ]

        def add_above_and_below(batch):
            above_below[batch] = sums.tile([P, batch[2] * VECTOR_PIXELS], F32, name="above_below")
            nc.vector.tensor_tensor(
                out=rows_of(above_below[batch][:]), in0=padded_rows(batch, 0), in1=padded_rows(batch, 2), op=ADD
            )

        def add_centre(batch):
            nc.vector.tensor_tensor(
                out=column_sums(batch, 1), in0=rows_of(above_below[batch][:]), in1=padded_rows(batch, 1), op=ADD
            )

        def add_left_and_right(batch):
            left_right[batch] = sums.tile([P, batch[2] * VECTOR_PIXELS], F32, name="left_right")
            nc.vector.tensor_tensor(
                out=rows_of(left_right[batch][:]), in0=column_sums(batch, 0), in1=column_sums(batch, 2), op=ADD
            )

        def add_up_and_round(batch):
            b, first, banks = batch
            rounded = nbrs.tile([P, banks * VECTOR_PIXELS], BF16, name="rounded")
            nc.vector.tensor_tensor(out=rounded[:], in0=left_right[batch][:], in1=above_below[batch][:], op=ADD)
            for g in range(banks):
                nbr[b, first + g] = rounded[:, g * VECTOR_PIXELS : (g + 1) * VECTOR_PIXELS]

        add_steps = [add_above_and_below, add_centre, add_left_and_right, add_up_and_round]

        def copy_strip(b, s, first, count):
            if b not in strips:
                strips[b] = strip_pool.tile([P, STRIPS, SIDE, PATCH_COLS], BF16, name="strips")
            nc.vector.tensor_copy(
                out=strips[b][:, s, first : first + count, :],
                in_=x_pad[:, b, first : first + count, s * STRIP_STEP : s * STRIP_STEP + PATCH_COLS],
            )

        def transpose_patches(k):
            b, part = divmod(k, CHUNKS_PER_IMAGE)
            for h in range(BANKS_PER_CHUNK):
                flipped[k, h] = psum_flip.tile([P, STRIPS, P], BF16, name="flipped")
                first = part * CHUNK_ROWS + h * BANK_ROWS
                for s in range(STRIPS):
                    nc.tensor.transpose(
                        flipped[k, h][:, s, :],
                        strips[b][:, s, first : first + PATCH_ROWS, :].rearrange("p i j -> p (i j)"),
                        ident[:],
                    )

        def sum_on_tensor_engine(k, h):
            blocks = patches.tile([P, STRIPS, P], BF16, name="blocks")
            nc.vector.tensor_copy(out=blocks[:], in_=flipped[k, h][:])
            nbr_acc[k, h] = psum_nbr.tile([P, TENSOR_ROWS, SIDE], F32, name="nbr_acc")
            for s in range(STRIPS):
                lo = 0 if s == 0 else 1
                hi = PATCH_COLS if s == STRIPS - 1 else STRIP_STEP + 1
                nc.tensor.matmul(
                    out=nbr_acc[k, h][:, :, s * STRIP_STEP + lo : s * STRIP_STEP + hi],
                    lhsT=blocks[:, s, :],
                    rhs=window[:, :, lo:hi],
                    start=True,
                    stop=True,
                )

        def spread_second_pass(k, h):
            nc.sync.dma_start(
                out=xn[k, h][:, BANK * PACK : PASSES * BANK * PACK],
                in_=xn[k, h][1::PASSES, 0 : BANK * PACK].unsqueeze(1).to_broadcast([PASS_CHANNELS, 2, BANK * PACK]),
            )

        def spread_first_pass(k, h):
            nc.sync.dma_start(out=xn[k, h][1::PASSES, 0 : BANK * PACK], in_=xn[k, h][0::PASSES, 0 : BANK * PACK])

        def repeat_tensor_rows(k, h):
            xn[k, h] = moving.tile([P, PASSES * BANK * PACK], BF16, name="xn", align_bytes=64)
            nc.scalar.copy(
                out=xn[k, h][:, 0 : TENSOR_PIXELS * PACK].rearrange("p (w t) -> p w t", t=PACK),
                in_=nbr_acc[k, h][:]
                .rearrange("p o j -> p (o j)")
                .unsqueeze(2)
                .to_broadcast([P, TENSOR_PIXELS, PACK]),
            )

        def repeat_vector_rows(k, h):
            copy = nc.vector.tensor_copy if k < QUANTISE_LAG else nc.scalar.copy
            copy(
                out=xn[k, h][:, TENSOR_PIXELS * PACK : BANK * PACK].rearrange("p (w t) -> p w t", t=PACK),
                in_=nbr[k // CHUNKS_PER_IMAGE, (k % CHUNKS_PER_IMAGE) * BANKS_PER_CHUNK + h]
                .unsqueeze(2)
                .to_broadcast([P, VECTOR_PIXELS, PACK]),
            )
            spread_second_pass(k, h)

        def quantise_and_multiply(k, h):
            codes = packed.tile([P, PASSES * BANK], U32, name="codes", align_bytes=64)
            planes = packed.tile([P, PASSES * BANK], U8, name="planes", align_bytes=64)
            nc.vector.quantize_mx(out=codes[:].bitcast(FP8X4), scales=planes[:], in_=xn[k, h][:])
            acc[k, h] = psum_acc.tile([HID, BANK], F32, name="acc")
            for g in range(PASSES):
                nc.tensor.matmul_mx(
                    out=acc[k, h][:],
                    lhsT=w_codes[:, g, :].bitcast(FP4X4),
                    lhsT_scale=w_planes[:, g, :],
                    rhs=codes[:, g * BANK : (g + 1) * BANK].bitcast(FP8X4),
                    rhs_scale=planes[:, g * BANK : (g + 1) * BANK],
                    start=(g == 0),
                    stop=(g == PASSES - 1),
                )

        def scalar_takes(k, h):
            return k >= N_CHUNKS - QUANTISE_LAG

        def exponentials(k):
            neg[k] = tails.tile([HID, CHUNK], F32, name="neg")
            for h in range(BANKS_PER_CHUNK):
                nc.scalar.activation(out=neg[k][:, h * BANK : (h + 1) * BANK], in_=acc[k, h][:], func=EXP)

        def negative_part(k, on_scalar):
            mine = [h for h in range(BANKS_PER_CHUNK) if scalar_takes(k, h) == on_scalar]
            if on_scalar:
                for h in mine:
                    part = neg[k][:, h * BANK : (h + 1) * BANK]
                    nc.scalar.activation(out=part, in_=part, func=RELU, bias=1.0, scale=-1.0)
            elif mine:
                part = neg[k][:, mine[0] * BANK : (mine[-1] + 1) * BANK]
                nc.vector.tensor_scalar(out=part, in0=part, scalar1=1.0, scalar2=-1.0, op0=MIN, op1=ADD)

        def finish(k, h):
            res = results.tile([HID, BANK], F32, name="res")
            nc.vector.scalar_tensor_tensor(
                out=res[:],
                in0=neg[k][:, h * BANK : (h + 1) * BANK],
                scalar=-1.0 if scalar_takes(k, h) else 1.0,
                in1=acc[k, h][:],
                op0=MULT,
                op1=MAX,
            )
            b, part = divmod(k, CHUNKS_PER_IMAGE)
            bank_rows = BANK // SIDE
            first = part * CHUNK_ROWS + h * bank_rows
            nc.sync.dma_start(out=out[b, :, first : first + bank_rows, :].rearrange("o i j -> o (i j)"), in_=res[:])

        def whole_sums(j):
            if j < 2:
                return [(0, (2 * j + i) * BANKS_PER_CHUNK, BANKS_PER_CHUNK) for i in range(2)]
            return []

        def single_adds(j):
            if j in (2, 3):
                first = 2 * (j - 2)
                return [(0, (add_steps[first], (1, 0, BANKS_PER_IMAGE))), (2, (add_steps[first + 1], (1, 0, BANKS_PER_IMAGE)))]
            b, stage = divmod(j + CHUNKS_PER_IMAGE, CHUNKS_PER_IMAGE)
            if 2 <= b < IMAGES:
                return [(1, (add_steps[stage], (b, 0, BANKS_PER_IMAGE)))]
            return []

        with tc.manual_schedule():
            for s in range(STRIPS):
                copy_strip(0, s, 0, CHUNK_ROWS)
            transpose_patches(0)
            for j in range(N_CHUNKS + FINISH_LAG):
                repeating = j < N_CHUNKS
                q = j - QUANTISE_LAG
                quantising = 0 <= q < N_CHUNKS
                f = j - FINISH_LAG
                finishing = 0 <= f
                summed = whole_sums(j)
                singles = single_adds(j)
                for batch in summed:
                    add_above_and_below(batch)
                for place, (step, batch) in singles:
                    if place == 0:
                        step(batch)
                if quantising:
                    quantise_and_multiply(q, 0)
                if finishing:
                    negative_part(f, False)
                for batch in summed[0:1]:
                    add_centre(batch)
                for place, (step, batch) in singles:
                    if place == 1:
                        step(batch)
                if quantising:
                    quantise_and_multiply(q, 1)
                    exponentials(q)
                    negative_part(q, True)
                for batch in summed[0:1]:
                    add_left_and_right(batch)
                if repeating:
                    for h in range(BANKS_PER_CHUNK):
                        sum_on_tensor_engine(j, h)
                        repeat_tensor_rows(j, h)
                if finishing:
                    finish(f, 0)
                    finish(f, 1)
                for batch in summed[0:1]:
                    add_up_and_round(batch)
                for batch in summed[1:2]:
                    add_centre(batch)
                for place, (step, batch) in singles:
                    if place == 2:
                        step(batch)
                if repeating:
                    repeat_vector_rows(j, 0)
                for batch in summed[1:2]:
                    add_left_and_right(batch)
                if repeating:
                    repeat_vector_rows(j, 1)
                    for h in range(BANKS_PER_CHUNK):
                        spread_first_pass(j, h)
                for batch in summed[1:2]:
                    add_up_and_round(batch)
                if j == 0:
                    for s in range(STRIPS):
                        copy_strip(0, s, CHUNK_ROWS, SIDE - CHUNK_ROWS)
                b, part = divmod(j, CHUNKS_PER_IMAGE)
                if b + 1 < IMAGES:
                    for s in range(STRIPS):
                        if min(s, CHUNKS_PER_IMAGE - 1) == part:
                            copy_strip(b + 1, s, 0, SIDE)
                if j + 1 < N_CHUNKS:
                    transpose_patches(j + 1)
